import numpy as np
import ml_dtypes


def mxq(x, axis, fmt="e4m3"):
    dtype, down = {"e4m3": (ml_dtypes.float8_e4m3fn, 7), "e5m2": (ml_dtypes.float8_e5m2, 14)}[fmt]
    v = np.moveaxis(np.asarray(x, np.float32).astype(ml_dtypes.bfloat16).astype(np.float64), axis, -1)
    blocks = v.reshape(v.shape[:-1] + (-1, 32))
    amax = np.abs(blocks).max(-1, keepdims=True)
    byte = np.maximum(np.where(amax > 0, np.frexp(amax)[1] - 1 + 127, 0) - down, 1)
    scale = np.exp2(byte - 127.0)
    codes = (blocks / scale).astype(np.float32).astype(dtype).astype(np.float64)
    return np.moveaxis((codes * scale).reshape(v.shape), -1, axis)


WIDE = False


def mx_kscale(k):
    if not WIDE:
        return np.ones(k)
    levels = np.array([10, -10, 5, -5, 0])
    a = np.random.permutation(np.resize(levels, k // 512 * 4)).reshape(k // 512, 4)
    idx = np.arange(k)
    return np.exp2(a[idx // 512, idx % 128 // 32])


BF16 = ml_dtypes.bfloat16


def bf(x):
    return np.asarray(x, np.float32).astype(BF16)


def f64(x):
    return np.asarray(x).astype(np.float64)


N, C, O, TH, TW = 2, 512, 512, 16, 32
BN_EPS = 1e-5
IMG_SIZES = [(max(TH >> (l + 1), 1), max(TW >> (l + 1), 1)) for l in range(5)]


def setup_inputs():
    s = mx_kscale(C)
    sc = s[None, :, None, None]
    inp = {}
    for l, (h, w) in enumerate(IMG_SIZES):
        inp[f'img_feat{l}'] = bf(np.random.standard_normal((N, C, h, w)) * 0.5 * sc)
    inp['pts_feat0'] = bf(np.random.standard_normal((N, C, TH, TW)) * sc)
    inp['img_w'] = bf(np.random.standard_normal((O, C)) / np.sqrt(C) / s[None, :])
    inp['img_b'] = bf(np.random.standard_normal(O) * 0.1)
    inp['img_gamma'] = bf(1.0 + 0.1 * np.random.standard_normal(O))
    inp['img_beta'] = bf(np.random.standard_normal(O) * 0.1)
    inp['img_mean'] = bf(np.random.standard_normal(O) * 0.1)
    inp['img_var'] = bf(np.random.uniform(0.5, 1.5, O))
    inp['pts_w'] = bf(np.random.standard_normal((O, C)) / np.sqrt(C) / s[None, :])
    inp['pts_b'] = bf(np.random.standard_normal(O) * 0.1)
    inp['pts_gamma'] = bf(1.0 + 0.1 * np.random.standard_normal(O))
    inp['pts_beta'] = bf(np.random.standard_normal(O) * 0.1)
    inp['pts_mean'] = bf(np.random.standard_normal(O) * 0.1)
    inp['pts_var'] = bf(np.random.uniform(0.5, 1.5, O))
    return inp


def _obtain_mlvl(feats, th, tw):
    n = feats[0].shape[0]
    outs = []
    for i in range(n):
        acc = None
        for lvl, f in enumerate(feats):
            x = f[i]
            if lvl > 0:
                s = i + 1
                x = np.repeat(np.repeat(x, s, axis=1), s, axis=2)
            dh = th - x.shape[1]
            dw = tw - x.shape[2]
            x = np.pad(x, ((0, 0), (dh // 2, dh - dh // 2), (dw // 2, dw - dw // 2)), mode='edge')
            acc = x if acc is None else acc + x
        outs.append(acc)
    return np.stack(outs, 0)


def _conv_bn_relu(x, w, b, gamma, beta, mean, var):
    n, c, h, wd = x.shape
    y = (mxq(w, 1, 'e4m3') @ mxq(x, 1, 'e4m3').reshape(n, c, h * wd)).reshape(n, -1, h, wd) + b[None, :, None, None]
    scale = gamma / np.sqrt(var + BN_EPS)
    y = (y - mean[None, :, None, None]) * scale[None, :, None, None] + beta[None, :, None, None]
    return np.maximum(y, 0.0)


def reference(img_feat0, img_feat1, img_feat2, img_feat3, img_feat4, pts_feat0,
              img_w, img_b, img_gamma, img_beta, img_mean, img_var,
              pts_w, pts_b, pts_gamma, pts_beta, pts_mean, pts_var):
    th, tw = pts_feat0.shape[2], pts_feat0.shape[3]
    pts_m = _obtain_mlvl([f64(pts_feat0)], th, tw)
    pts_pre = _conv_bn_relu(pts_m, f64(pts_w), f64(pts_b), f64(pts_gamma), f64(pts_beta), f64(pts_mean), f64(pts_var))
    img_m = _obtain_mlvl([f64(img_feat0), f64(img_feat1), f64(img_feat2), f64(img_feat3), f64(img_feat4)], th, tw)
    img_pre = _conv_bn_relu(img_m, f64(img_w), f64(img_b), f64(img_gamma), f64(img_beta), f64(img_mean), f64(img_var))
    return np.concatenate((img_pre, pts_pre), axis=1)

@@ -1,0 +1,218 @@
+from contextlib import ExitStack
+
+import concourse.mybir as mybir
+from concourse.masks import make_identity
+
+F32 = mybir.dt.float32
+BF16 = mybir.dt.bfloat16
+U32 = mybir.dt.uint32
+U8 = mybir.dt.uint8
+FP8X4 = mybir.dt.float8_e4m3fn_x4
+ADD = mybir.AluOpType.add
+SUB = mybir.AluOpType.subtract
+MUL = mybir.AluOpType.mult
+ACT = mybir.ActivationFunctionType
+
+P = 128
+NS = 2
+C = 512
+O = 512
+OT = O // P
+HW = 512
+BN_EPS = 1e-5
+FLOPS = 2 * 2 * O * C * NS * HW
+
+
+def tile_prefusioncat_kernel(
+    tc,
+    img_feat0, img_feat1, img_feat2, img_feat3, img_feat4, pts_feat0,
+    img_w, img_b, img_gamma, img_beta, img_mean, img_var,
+    pts_w, pts_b, pts_gamma, pts_beta, pts_mean, pts_var,
+    out,
+):
+    nc = tc.nc
+    out_v = out.rearrange("n o h w -> n o (h w)")
+    with ExitStack() as ctx:
+        keep = ctx.enter_context(tc.tile_pool(name="keep", bufs=1))
+        ypool = ctx.enter_context(tc.tile_pool(name="ypool", bufs=4))
+        psw = ctx.enter_context(tc.psum_pool(name="psw", bufs=2))
+        pso = ctx.enter_context(tc.psum_pool(name="pso", bufs=4))
+        psm = ctx.enter_context(tc.psum_pool(name="psm", bufs=1))
+
+        ident_f = keep.tile([P, P], F32, name="ident_f")
+        make_identity(nc, ident_f[:])
+        ident_b = keep.tile([P, P], BF16, name="ident_b")
+        make_identity(nc, ident_b[:])
+        one = keep.tile([P, 1], F32, name="one")
+        nc.vector.memset(one[:], 1.0)
+        warm = keep.tile([P, 1], F32, name="warm")
+        nc.scalar.activation(out=warm[:], in_=one[:], func=ACT.Sqrt)
+        prow = keep.tile([P, P], BF16, name="prow")
+        nc.vector.memset(prow[:], 0.0)
+
+        w_raw = {}
+        for br, w in (("pts", pts_w), ("img", img_w)):
+            w_raw[br] = keep.tile([P, OT, C], BF16, name="w_raw_" + br)
+        x_raw = [keep.tile([P, 4, HW], BF16, name="x_raw%d" % n) for n in range(NS)]
+        nc.sync.dma_start(out=w_raw["pts"][:], in_=pts_w.rearrange("(a p) c -> p a c", p=P))
+        for n in range(NS):
+            nc.sync.dma_start(out=x_raw[n][:], in_=pts_feat0[n].rearrange("(p t) h w -> p t (h w)", t=4))
+        sizes = (128, 32, 8, 2, 1)
+        feats = (img_feat0, img_feat1, img_feat2, img_feat3, img_feat4)
+        f_raw = []
+        for lvl in range(5):
+            ft = keep.tile([P, 2 * 4, sizes[lvl]], BF16, name="f_raw%d" % lvl)
+            nc.sync.dma_start(
+                out=ft[:].rearrange("p (n t) s -> p n (t s)", n=NS),
+                in_=feats[lvl].rearrange("n (p t) h w -> p n (t h w)", t=4),
+            )
+            f_raw.append(ft)
+        nc.sync.dma_start(out=w_raw["img"][:], in_=img_w.rearrange("(a p) c -> p a c", p=P))
+        params = (
+            (pts_b, img_b), (pts_gamma, img_gamma), (pts_beta, img_beta),
+            (pts_mean, img_mean), (pts_var, img_var),
+        )
+        for q in range(5):
+            for b in range(2):
+                r0 = (q * 2 + b) * OT
+                nc.scalar.dma_start(out=prow[r0:r0 + OT, :], in_=params[q][b].rearrange("(a p) -> a p", p=P))
+
+        pt_ps = psm.tile([P, P], BF16, name="pt_ps")
+        nc.tensor.transpose(pt_ps[:], prow[:], ident_b[:])
+        pf = keep.tile([P, 5, 8], F32, name="pf")
+        nc.vector.tensor_copy(out=pf[:].rearrange("p q j -> p (q j)"), in_=pt_ps[:, 0:40])
+        ve = keep.tile([P, 8], F32, name="ve")
+        nc.vector.tensor_scalar_add(out=ve[:], in0=pf[:, 4, :], scalar1=BN_EPS)
+        sd = keep.tile([P, 8], F32, name="sd")
+        nc.scalar.activation(out=sd[:], in_=ve[:], func=ACT.Sqrt)
+        rs = keep.tile([P, 8], F32, name="rs")
+        nc.vector.reciprocal(out=rs[:], in_=sd[:])
+        bn_s = keep.tile([P, 8], F32, name="bn_s")
+        nc.vector.tensor_tensor(out=bn_s[:], in0=pf[:, 1, :], in1=rs[:], op=MUL)
+        dm = keep.tile([P, 8], F32, name="dm")
+        nc.vector.tensor_tensor(out=dm[:], in0=pf[:, 0, :], in1=pf[:, 3, :], op=SUB)
+        ds = keep.tile([P, 8], F32, name="ds")
+        nc.vector.tensor_tensor(out=ds[:], in0=dm[:], in1=bn_s[:], op=MUL)
+        bn_t = keep.tile([P, 8], F32, name="bn_t")
+        nc.vector.tensor_tensor(out=bn_t[:], in0=ds[:], in1=pf[:, 2, :], op=ADD)
+
+        def weight_path(br):
+            words = w_raw[br][:].bitcast(F32).rearrange("p a (m u) -> p a u m", u=2)
+            wg = keep.tile([P, OT * P * 4], BF16, name="wg_" + br, align_bytes=64)
+            wg_w = wg[:].bitcast(F32).rearrange("p (a o u) -> p a o u", a=OT, u=2)
+            for h in range(2):
+                wt = psw.tile([P, 2, 2, P], F32, name="wt")
+                for a in range(2):
+                    for u in range(2):
+                        nc.tensor.transpose(wt[:, a, u, :], words[:, 2 * h + a, u, :], ident_f[:])
+                nc.scalar.copy(out=wg_w[:, 2 * h:2 * h + 2], in_=wt[:].rearrange("p a u o -> p a o u"))
+            wq = keep.tile([P, O], U32, name="wq_" + br, align_bytes=64)
+            ws = keep.tile([P, O], U8, name="ws_" + br, align_bytes=64)
+            nc.vector.quantize_mx(out=wq[:].bitcast(FP8X4), scales=ws[:], in_=wg[:])
+            return wq, ws
+
+        wq, ws = weight_path("pts")
+        for n in range(NS):
+            xg = keep.tile([P, HW, 4], BF16, name="xg%d" % n, align_bytes=64)
+            nc.vector.tensor_copy(
+                out=xg[:].rearrange("p (c i) t -> p c t i", i=4),
+                in_=x_raw[n][:].rearrange("p t (c i) -> p c t i", i=4),
+            )
+            xq = keep.tile([P, HW], U32, name="xq%d" % n, align_bytes=64)
+            xs = keep.tile([P, HW], U8, name="xs%d" % n, align_bytes=64)
+            nc.vector.quantize_mx(out=xq[:].bitcast(FP8X4), scales=xs[:], in_=xg[:].rearrange("p c t -> p (c t)"))
+            for a in range(OT):
+                acc = pso.tile([P, HW], F32, name="acc")
+                nc.tensor.matmul_mx(
+                    out=acc[:],
+                    lhsT=wq[:, a * P:(a + 1) * P].bitcast(FP8X4), lhsT_scale=ws[:, a * P:(a + 1) * P],
+                    rhs=xq[:].bitcast(FP8X4), rhs_scale=xs[:],
+                    start=True, stop=True,
+                )
+                y = ypool.tile([P, HW], F32, name="y")
+                nc.scalar.activation(out=y[:], in_=acc[:], func=ACT.Relu, bias=bn_t[:, a:a + 1], scale=bn_s[:, a:a + 1])
+                nc.sync.dma_start(out=out_v[n, O + a * P:O + (a + 1) * P, :], in_=y[:])
+
+        f0, f1, f2, f3, f4 = f_raw
+        g3x = keep.tile([P, 8, 2, 2], F32, name="g3x")
+        nc.vector.tensor_tensor(
+            out=g3x[:], in0=f3[:].unsqueeze(3).to_broadcast([P, 8, 2, 2]),
+            in1=f4[:].unsqueeze(3).to_broadcast([P, 8, 2, 2]), op=ADD,
+        )
+        g2 = keep.tile([P, 8, 2, 4], F32, name="g2")
+        nc.vector.tensor_tensor(
+            out=g2[:], in0=f2[:].rearrange("p q (a b) -> p q a b", a=2),
+            in1=g3x[:].rearrange("p q b e -> p q (b e)").unsqueeze(2).to_broadcast([P, 8, 2, 4]), op=ADD,
+        )
+        g1 = keep.tile([P, 8, 4, 8], F32, name="g1")
+        g1v = g1[:].rearrange("p q (a e) b -> p (q a) e b", e=2)
+        f1v = f1[:].rearrange("p q (a e b) -> p (q a) e b", e=2, b=8)
+        g2v = g2[:].rearrange("p q a b -> p (q a) b")
+        nc.vector.tensor_tensor(
+            out=g1v[:, :, :, 2:6], in0=f1v[:, :, :, 2:6],
+            in1=g2v.unsqueeze(2).to_broadcast([P, 16, 2, 4]), op=ADD,
+        )
+        nc.vector.tensor_tensor(
+            out=g1v[:, :, :, 0:2], in0=f1v[:, :, :, 0:2],
+            in1=g2v[:, :, 0:1].unsqueeze(2).to_broadcast([P, 16, 2, 2]), op=ADD,
+        )
+        nc.vector.tensor_tensor(
+            out=g1v[:, :, :, 6:8], in0=f1v[:, :, :, 6:8],
+            in1=g2v[:, :, 3:4].unsqueeze(2).to_broadcast([P, 16, 2, 2]), op=ADD,
+        )
+        core = keep.tile([P, 8, P], BF16, name="core")
+        p0 = keep.tile([P, 4, 4, 16], F32, name="p0")
+        p0v = p0[:].rearrange("p t a s -> p (t a) s")
+        g1s0 = g1[:, 0:4].rearrange("p t a b -> p (t a) b")
+        nc.vector.tensor_copy(out=p0v[:, :, 4:12], in_=g1s0)
+        nc.vector.tensor_copy(out=p0v[:, :, 0:4], in_=g1s0[:, :, 0:1].to_broadcast([P, 16, 4]))
+        nc.vector.tensor_copy(out=p0v[:, :, 12:16], in_=g1s0[:, :, 7:8].to_broadcast([P, 16, 4]))
+        c0 = core[:, 0:4].rearrange("p t (r s) -> p t r s", s=16)
+        f00 = f0[:, 0:4].rearrange("p t (r s) -> p t r s", s=16)
+        nc.vector.tensor_tensor(out=c0[:, :, 2:6, :], in0=f00[:, :, 2:6, :], in1=p0[:], op=ADD)
+        nc.vector.tensor_tensor(
+            out=c0[:, :, 0:2, :], in0=f00[:, :, 0:2, :], in1=p0[:, :, 0:1, :].to_broadcast([P, 4, 2, 16]), op=ADD,
+        )
+        nc.vector.tensor_tensor(
+            out=c0[:, :, 6:8, :], in0=f00[:, :, 6:8, :], in1=p0[:, :, 3:4, :].to_broadcast([P, 4, 2, 16]), op=ADD,
+        )
+        c1 = core[:, 4:8].rearrange("p t (a e b d) -> p (t a) e b d", e=2, b=8, d=2)
+        f01 = f0[:, 4:8].rearrange("p t (a e b d) -> p (t a) e b d", e=2, b=8, d=2)
+        g1s1 = g1[:, 4:8].rearrange("p t a b -> p (t a) b").unsqueeze(3).to_broadcast([P, 16, 8, 2])
+        for e in range(2):
+            nc.vector.tensor_tensor(out=c1[:, :, e], in0=f01[:, :, e], in1=g1s1, op=ADD)
+        cg = keep.tile([P, NS, P, 4], BF16, name="cg", align_bytes=64)
+        nc.vector.tensor_copy(out=cg[:], in_=core[:].rearrange("p (n t) c -> p n c t", n=NS))
+        cq = keep.tile([P, NS * P], U32, name="cq", align_bytes=64)
+        cs = keep.tile([P, NS * P], U8, name="cs", align_bytes=64)
+        nc.vector.quantize_mx(out=cq[:].bitcast(FP8X4), scales=cs[:], in_=cg[:].rearrange("p n c t -> p (n c t)"))
+
+        wq, ws = weight_path("img")
+        fi = keep.tile([P, OT, NS, 16, 32], F32, name="fi")
+        for h in range(2):
+            acc = pso.tile([P, 2, NS * P], F32, name="acc")
+            for k in range(2):
+                a = 2 * h + k
+                nc.tensor.matmul_mx(
+                    out=acc[:, k, :],
+                    lhsT=wq[:, a * P:(a + 1) * P].bitcast(FP8X4), lhsT_scale=ws[:, a * P:(a + 1) * P],
+                    rhs=cq[:].bitcast(FP8X4), rhs_scale=cs[:],
+                    start=True, stop=True,
+                )
+            for k in range(2):
+                a = 2 * h + k
+                nc.scalar.activation(
+                    out=fi[:, a, :, 4:12, 8:24], in_=acc[:, k, :].rearrange("p (n r s) -> p n r s", n=NS, s=16),
+                    func=ACT.Relu, bias=bn_t[:, 4 + a:5 + a], scale=bn_s[:, 4 + a:5 + a],
+                )
+            half = fi[:, 2 * h:2 * h + 2].rearrange("p a n r s -> p (a n) r s")
+            nc.vector.tensor_copy(out=half[:, :, 4:12, 0:8], in_=half[:, :, 4:12, 8:9].to_broadcast([P, 4, 8, 8]))
+            nc.vector.tensor_copy(out=half[:, :, 4:12, 24:32], in_=half[:, :, 4:12, 23:24].to_broadcast([P, 4, 8, 8]))
+            nc.vector.tensor_copy(out=half[:, :, 0:4, :], in_=half[:, :, 4:5, :].to_broadcast([P, 4, 4, 32]))
+            nc.vector.tensor_copy(out=half[:, :, 12:16, :], in_=half[:, :, 11:12, :].to_broadcast([P, 4, 4, 32]))
+            for k in range(2):
+                a = 2 * h + k
+                nc.sync.dma_start(
+                    out=out_v[:, a * P:(a + 1) * P, :].rearrange("n o s -> o n s"),
+                    in_=fi[:, a].rearrange("p n r s -> p n (r s)"),
+                )

@@ -31,108 +31,83 @@ def tile_prefusioncat_kernel(
     out,
 ):
     nc = tc.nc
-    out_v = out.rearrange("n o h w -> n o (h w)")
+    out_v = out.rearrange("n (b p a) h w -> n b p a (h w)", b=2, a=OT)
     with ExitStack() as ctx:
         keep = ctx.enter_context(tc.tile_pool(name="keep", bufs=1))
         ypool = ctx.enter_context(tc.tile_pool(name="ypool", bufs=4))
         psw = ctx.enter_context(tc.psum_pool(name="psw", bufs=2))
-        pso = ctx.enter_context(tc.psum_pool(name="pso", bufs=4))
-        psm = ctx.enter_context(tc.psum_pool(name="psm", bufs=1))
+        pso = ctx.enter_context(tc.psum_pool(name="pso", bufs=5))
+        ctx.enter_context(tc.manual_schedule())
 
         ident_f = keep.tile([P, P], F32, name="ident_f")
         make_identity(nc, ident_f[:])
-        ident_b = keep.tile([P, P], BF16, name="ident_b")
-        make_identity(nc, ident_b[:])
+
+        w_raw = {"pts": keep.tile([P, OT, C], BF16, name="w_raw_pts"), "img": keep.tile([P, OT, C], BF16, name="w_raw_img")}
+        x_raw = [keep.tile([P, 4, HW], BF16, name="x_raw%d" % n) for n in range(NS)]
+        sizes = (128, 32, 8, 2, 1)
+        feats = (img_feat0, img_feat1, img_feat2, img_feat3, img_feat4)
+        f_raw = [keep.tile([P, 2 * 4, sizes[lvl]], BF16, name="f_raw%d" % lvl) for lvl in range(5)]
+        par = {"pts": keep.tile([P, 5, 16], BF16, name="par_pts"), "img": keep.tile([P, 5, 16], BF16, name="par_img")}
+        vecs = {
+            "pts": (pts_var, pts_gamma, pts_b, pts_mean, pts_beta),
+            "img": (img_var, img_gamma, img_b, img_mean, img_beta),
+        }
+
+        def load_feat(eng, lvl):
+            eng.dma_start(
+                out=f_raw[lvl][:].rearrange("p (n t) s -> p n (t s)", n=NS),
+                in_=feats[lvl].rearrange("n (p t) h w -> p n (t h w)", t=4),
+            )
+
+        def load_par(eng, br, q):
+            eng.dma_start(out=par[br][:, q, 0:OT], in_=vecs[br][q].rearrange("(p a) -> p a", a=OT))
+
+        def load_x(n):
+            nc.sync.dma_start(out=x_raw[n][:], in_=pts_feat0[n].rearrange("(p t) h w -> p t (h w)", t=4))
+
+        img_w_v = img_w.rearrange("(p a) c -> p a c", a=OT)
+        load_feat(nc.sync, 4)
+        load_feat(nc.scalar, 2)
+        load_feat(nc.sync, 3)
+        load_feat(nc.scalar, 1)
+        load_par(nc.scalar, "img", 0)
+        load_feat(nc.sync, 0)
+        nc.sync.dma_start(out=w_raw["img"][:, 0:2, :], in_=img_w_v[:, 0:2, :])
+        nc.sync.dma_start(out=w_raw["img"][:, 2:4, :], in_=img_w_v[:, 2:4, :])
+        for q in range(1, 5):
+            load_par(nc.sync, "img", q)
+        nc.sync.dma_start(out=w_raw["pts"][:], in_=pts_w.rearrange("(p a) c -> p a c", a=OT))
+        load_x(0)
+        for q in range(5):
+            load_par(nc.sync, "pts", q)
+        load_x(1)
+
         one = keep.tile([P, 1], F32, name="one")
         nc.vector.memset(one[:], 1.0)
         warm = keep.tile([P, 1], F32, name="warm")
         nc.scalar.activation(out=warm[:], in_=one[:], func=ACT.Sqrt)
-        prow = keep.tile([P, P], BF16, name="prow")
-        nc.vector.memset(prow[:], 0.0)
 
-        w_raw = {}
-        for br, w in (("pts", pts_w), ("img", img_w)):
-            w_raw[br] = keep.tile([P, OT, C], BF16, name="w_raw_" + br)
-        x_raw = [keep.tile([P, 4, HW], BF16, name="x_raw%d" % n) for n in range(NS)]
-        nc.sync.dma_start(out=w_raw["pts"][:], in_=pts_w.rearrange("(a p) c -> p a c", p=P))
-        for n in range(NS):
-            nc.sync.dma_start(out=x_raw[n][:], in_=pts_feat0[n].rearrange("(p t) h w -> p t (h w)", t=4))
-        sizes = (128, 32, 8, 2, 1)
-        feats = (img_feat0, img_feat1, img_feat2, img_feat3, img_feat4)
-        f_raw = []
-        for lvl in range(5):
-            ft = keep.tile([P, 2 * 4, sizes[lvl]], BF16, name="f_raw%d" % lvl)
-            nc.sync.dma_start(
-                out=ft[:].rearrange("p (n t) s -> p n (t s)", n=NS),
-                in_=feats[lvl].rearrange("n (p t) h w -> p n (t h w)", t=4),
-            )
-            f_raw.append(ft)
-        nc.sync.dma_start(out=w_raw["img"][:], in_=img_w.rearrange("(a p) c -> p a c", p=P))
-        params = (
-            (pts_b, img_b), (pts_gamma, img_gamma), (pts_beta, img_beta),
-            (pts_mean, img_mean), (pts_var, img_var),
-        )
-        for q in range(5):
-            for b in range(2):
-                r0 = (q * 2 + b) * OT
-                nc.scalar.dma_start(out=prow[r0:r0 + OT, :], in_=params[q][b].rearrange("(a p) -> a p", p=P))
+        bn = {}
 
-        pt_ps = psm.tile([P, P], BF16, name="pt_ps")
-        nc.tensor.transpose(pt_ps[:], prow[:], ident_b[:])
-        pf = keep.tile([P, 5, 8], F32, name="pf")
-        nc.vector.tensor_copy(out=pf[:].rearrange("p q j -> p (q j)"), in_=pt_ps[:, 0:40])
-        ve = keep.tile([P, 8], F32, name="ve")
-        nc.vector.tensor_scalar_add(out=ve[:], in0=pf[:, 4, :], scalar1=BN_EPS)
-        sd = keep.tile([P, 8], F32, name="sd")
-        nc.scalar.activation(out=sd[:], in_=ve[:], func=ACT.Sqrt)
-        rs = keep.tile([P, 8], F32, name="rs")
-        nc.vector.reciprocal(out=rs[:], in_=sd[:])
-        bn_s = keep.tile([P, 8], F32, name="bn_s")
-        nc.vector.tensor_tensor(out=bn_s[:], in0=pf[:, 1, :], in1=rs[:], op=MUL)
-        dm = keep.tile([P, 8], F32, name="dm")
-        nc.vector.tensor_tensor(out=dm[:], in0=pf[:, 0, :], in1=pf[:, 3, :], op=SUB)
-        ds = keep.tile([P, 8], F32, name="ds")
-        nc.vector.tensor_tensor(out=ds[:], in0=dm[:], in1=bn_s[:], op=MUL)
-        bn_t = keep.tile([P, 8], F32, name="bn_t")
-        nc.vector.tensor_tensor(out=bn_t[:], in0=ds[:], in1=pf[:, 2, :], op=ADD)
+        def bn_tile(br, nm):
+            bn[(br, nm)] = keep.tile([P, OT], F32, name=nm + "_" + br)
+            return bn[(br, nm)]
 
-        def weight_path(br):
-            words = w_raw[br][:].bitcast(F32).rearrange("p a (m u) -> p a u m", u=2)
-            wg = keep.tile([P, OT * P * 4], BF16, name="wg_" + br, align_bytes=64)
-            wg_w = wg[:].bitcast(F32).rearrange("p (a o u) -> p a o u", a=OT, u=2)
-            for h in range(2):
-                wt = psw.tile([P, 2, 2, P], F32, name="wt")
-                for a in range(2):
-                    for u in range(2):
-                        nc.tensor.transpose(wt[:, a, u, :], words[:, 2 * h + a, u, :], ident_f[:])
-                nc.scalar.copy(out=wg_w[:, 2 * h:2 * h + 2], in_=wt[:].rearrange("p a u o -> p a o u"))
-            wq = keep.tile([P, O], U32, name="wq_" + br, align_bytes=64)
-            ws = keep.tile([P, O], U8, name="ws_" + br, align_bytes=64)
-            nc.vector.quantize_mx(out=wq[:].bitcast(FP8X4), scales=ws[:], in_=wg[:])
-            return wq, ws
+        def bn_head(br):
+            nc.vector.tensor_scalar_add(out=bn_tile(br, "ve")[:], in0=par[br][:, 0, 0:OT], scalar1=BN_EPS)
+            nc.scalar.activation(out=bn_tile(br, "sd")[:], in_=bn[(br, "ve")][:], func=ACT.Sqrt)
 
-        wq, ws = weight_path("pts")
-        for n in range(NS):
-            xg = keep.tile([P, HW, 4], BF16, name="xg%d" % n, align_bytes=64)
-            nc.vector.tensor_copy(
-                out=xg[:].rearrange("p (c i) t -> p c t i", i=4),
-                in_=x_raw[n][:].rearrange("p t (c i) -> p c t i", i=4),
-            )
-            xq = keep.tile([P, HW], U32, name="xq%d" % n, align_bytes=64)
-            xs = keep.tile([P, HW], U8, name="xs%d" % n, align_bytes=64)
-            nc.vector.quantize_mx(out=xq[:].bitcast(FP8X4), scales=xs[:], in_=xg[:].rearrange("p c t -> p (c t)"))
-            for a in range(OT):
-                acc = pso.tile([P, HW], F32, name="acc")
-                nc.tensor.matmul_mx(
-                    out=acc[:],
-                    lhsT=wq[:, a * P:(a + 1) * P].bitcast(FP8X4), lhsT_scale=ws[:, a * P:(a + 1) * P],
-                    rhs=xq[:].bitcast(FP8X4), rhs_scale=xs[:],
-                    start=True, stop=True,
-                )
-                y = ypool.tile([P, HW], F32, name="y")
-                nc.scalar.activation(out=y[:], in_=acc[:], func=ACT.Relu, bias=bn_t[:, a:a + 1], scale=bn_s[:, a:a + 1])
-                nc.sync.dma_start(out=out_v[n, O + a * P:O + (a + 1) * P, :], in_=y[:])
+        def bn_mid(br):
+            nc.vector.reciprocal(out=bn_tile(br, "rs")[:], in_=bn[(br, "sd")][:])
 
+        def bn_tail(br):
+            pv = par[br]
+            nc.vector.tensor_tensor(out=bn_tile(br, "s")[:], in0=pv[:, 1, 0:OT], in1=bn[(br, "rs")][:], op=MUL)
+            nc.vector.tensor_tensor(out=bn_tile(br, "dm")[:], in0=pv[:, 2, 0:OT], in1=pv[:, 3, 0:OT], op=SUB)
+            nc.vector.tensor_tensor(out=bn_tile(br, "ds")[:], in0=bn[(br, "dm")][:], in1=bn[(br, "s")][:], op=MUL)
+            nc.vector.tensor_tensor(out=bn_tile(br, "t")[:], in0=bn[(br, "ds")][:], in1=pv[:, 4, 0:OT], op=ADD)
+
+        bn_head("img")
         f0, f1, f2, f3, f4 = f_raw
         g3x = keep.tile([P, 8, 2, 2], F32, name="g3x")
         nc.vector.tensor_tensor(
@@ -144,6 +119,7 @@ def tile_prefusioncat_kernel(
             out=g2[:], in0=f2[:].rearrange("p q (a b) -> p q a b", a=2),
             in1=g3x[:].rearrange("p q b e -> p q (b e)").unsqueeze(2).to_broadcast([P, 8, 2, 4]), op=ADD,
         )
+        bn_mid("img")
         g1 = keep.tile([P, 8, 4, 8], F32, name="g1")
         g1v = g1[:].rearrange("p q (a e) b -> p (q a) e b", e=2)
         f1v = f1[:].rearrange("p q (a e b) -> p (q a) e b", e=2, b=8)
@@ -160,59 +136,173 @@ def tile_prefusioncat_kernel(
             out=g1v[:, :, :, 6:8], in0=f1v[:, :, :, 6:8],
             in1=g2v[:, :, 3:4].unsqueeze(2).to_broadcast([P, 16, 2, 2]), op=ADD,
         )
-        core = keep.tile([P, 8, P], BF16, name="core")
-        p0 = keep.tile([P, 4, 4, 16], F32, name="p0")
-        p0v = p0[:].rearrange("p t a s -> p (t a) s")
-        g1s0 = g1[:, 0:4].rearrange("p t a b -> p (t a) b")
-        nc.vector.tensor_copy(out=p0v[:, :, 4:12], in_=g1s0)
-        nc.vector.tensor_copy(out=p0v[:, :, 0:4], in_=g1s0[:, :, 0:1].to_broadcast([P, 16, 4]))
-        nc.vector.tensor_copy(out=p0v[:, :, 12:16], in_=g1s0[:, :, 7:8].to_broadcast([P, 16, 4]))
-        c0 = core[:, 0:4].rearrange("p t (r s) -> p t r s", s=16)
-        f00 = f0[:, 0:4].rearrange("p t (r s) -> p t r s", s=16)
-        nc.vector.tensor_tensor(out=c0[:, :, 2:6, :], in0=f00[:, :, 2:6, :], in1=p0[:], op=ADD)
-        nc.vector.tensor_tensor(
-            out=c0[:, :, 0:2, :], in0=f00[:, :, 0:2, :], in1=p0[:, :, 0:1, :].to_broadcast([P, 4, 2, 16]), op=ADD,
+        ex = keep.tile([P, 8, 8, 16], F32, name="ex")
+        ex0 = ex[:, 0:4]
+        g10 = g1[:, 0:4]
+        nc.vector.tensor_copy(out=ex0[:, :, 2:6, 4:12], in_=g10)
+        nc.vector.tensor_copy(
+            out=ex0.rearrange("p t r (j c) -> p t r j c", c=4)[:, :, 2:6, 0:4:3, :],
+            in_=g10[:, :, :, 0:8:7].unsqueeze(4).to_broadcast([P, 4, 4, 2, 4]),
         )
-        nc.vector.tensor_tensor(
-            out=c0[:, :, 6:8, :], in0=f00[:, :, 6:8, :], in1=p0[:, :, 3:4, :].to_broadcast([P, 4, 2, 16]), op=ADD,
+        nc.vector.tensor_copy(
+            out=ex[:, 4:8].rearrange("p t (a e) (b d) -> p (t a) e b d", e=2, d=2),
+            in_=g1[:, 4:8].rearrange("p t a b -> p (t a) b").unsqueeze(2).unsqueeze(4).to_broadcast([P, 16, 2, 8, 2]),
         )
-        c1 = core[:, 4:8].rearrange("p t (a e b d) -> p (t a) e b d", e=2, b=8, d=2)
-        f01 = f0[:, 4:8].rearrange("p t (a e b d) -> p (t a) e b d", e=2, b=8, d=2)
-        g1s1 = g1[:, 4:8].rearrange("p t a b -> p (t a) b").unsqueeze(3).to_broadcast([P, 16, 8, 2])
-        for e in range(2):
-            nc.vector.tensor_tensor(out=c1[:, :, e], in0=f01[:, :, e], in1=g1s1, op=ADD)
+        nc.vector.tensor_copy(
+            out=ex0.rearrange("p t (j c) s -> p t j c s", c=2)[:, :, 0:4:3, :, :],
+            in_=ex0[:, :, 2:6:3, :].unsqueeze(3).to_broadcast([P, 4, 2, 2, 16]),
+        )
+
+        wt_ps = {}
+        wgt = {}
+        for br in ("pts", "img"):
+            wgt[br] = (
+                keep.tile([P, OT * P * 4], BF16, name="wg_" + br, align_bytes=64),
+                keep.tile([P, O], U32, name="wq_" + br, align_bytes=64),
+                keep.tile([P, O], U8, name="ws_" + br, align_bytes=64),
+            )
+
+        def w_transpose(br, h):
+            words = w_raw[br][:].bitcast(F32).rearrange("p a (m u) -> p a u m", u=2)
+            wt = psw.tile([P, 2, 2, P], F32, name="wt")
+            for a in range(2):
+                for u in range(2):
+                    nc.tensor.transpose(wt[:, a, u, :], words[:, 2 * h + a, u, :], ident_f[:])
+            wt_ps[(br, h)] = wt
+
+        def w_copy(br, h, copy_out):
+            wg_w = wgt[br][0][:].bitcast(F32).rearrange("p (a o u) -> p a o u", a=OT, u=2)
+            copy_out(out=wg_w[:, 2 * h:2 * h + 2], in_=wt_ps[(br, h)][:].rearrange("p a u o -> p a o u"))
+
+        def w_quant(br, lo, hi):
+            wg, wq, ws = wgt[br]
+            nc.vector.quantize_mx(
+                out=wq[:, lo * 256:hi * 256].bitcast(FP8X4), scales=ws[:, lo * 256:hi * 256],
+                in_=wg[:, lo * 1024:hi * 1024],
+            )
+
+        xt = [
+            (
+                keep.tile([P, HW, 4], BF16, name="xg%d" % n, align_bytes=64),
+                keep.tile([P, HW], U32, name="xq%d" % n, align_bytes=64),
+                keep.tile([P, HW], U8, name="xs%d" % n, align_bytes=64),
+            )
+            for n in range(NS)
+        ]
+
+        def x_regroup(n, copy_op, lo, hi):
+            copy_op(
+                out=xt[n][0][:, lo:hi, :].rearrange("p (c i) t -> p c t i", i=4),
+                in_=x_raw[n][:, :, lo:hi].rearrange("p t (c i) -> p c t i", i=4),
+            )
+
+        def x_quant(n):
+            xg, xq, xs = xt[n]
+            nc.vector.quantize_mx(out=xq[:].bitcast(FP8X4), scales=xs[:], in_=xg[:].rearrange("p c t -> p (c t)"))
+
+        def product(acc, br, a, rq, rs_):
+            wq, ws = wgt[br][1], wgt[br][2]
+            nc.tensor.matmul_mx(
+                out=acc,
+                lhsT=wq[:, a * P:(a + 1) * P].bitcast(FP8X4), lhsT_scale=ws[:, a * P:(a + 1) * P],
+                rhs=rq[:].bitcast(FP8X4), rhs_scale=rs_[:],
+                start=True, stop=True,
+            )
+
+        def relu(br, a, dst, src):
+            nc.scalar.activation(
+                out=dst, in_=src, func=ACT.Relu,
+                bias=bn[(br, "t")][:, a:a + 1], scale=bn[(br, "s")][:, a:a + 1],
+            )
+
+        def pts_products(n):
+            accs = []
+            for a in range(OT):
+                acc = pso.tile([P, HW], F32, name="acc")
+                product(acc[:], "pts", a, xt[n][1], xt[n][2])
+                accs.append(acc)
+            return accs
+
+        def pts_finish(n, accs, tiles):
+            y = ypool.tile([P, 2, HW], F32, name="y")
+            for k, a in enumerate(tiles):
+                relu("pts", a, y[:, k, :], accs[a][:])
+            nc.sync.dma_start(out=out_v[n, 1, :, tiles[0]:tiles[-1] + 1, :], in_=y[:, 0:len(tiles), :])
+
         cg = keep.tile([P, NS, P, 4], BF16, name="cg", align_bytes=64)
-        nc.vector.tensor_copy(out=cg[:], in_=core[:].rearrange("p (n t) c -> p n c t", n=NS))
         cq = keep.tile([P, NS * P], U32, name="cq", align_bytes=64)
         cs = keep.tile([P, NS * P], U8, name="cs", align_bytes=64)
-        nc.vector.quantize_mx(out=cq[:].bitcast(FP8X4), scales=cs[:], in_=cg[:].rearrange("p n c t -> p (n c t)"))
+        img_acc = {}
+        img_out = {}
 
-        wq, ws = weight_path("img")
-        fi = keep.tile([P, OT, NS, 16, 32], F32, name="fi")
-        for h in range(2):
+        def img_products(h):
             acc = pso.tile([P, 2, NS * P], F32, name="acc")
             for k in range(2):
-                a = 2 * h + k
-                nc.tensor.matmul_mx(
-                    out=acc[:, k, :],
-                    lhsT=wq[:, a * P:(a + 1) * P].bitcast(FP8X4), lhsT_scale=ws[:, a * P:(a + 1) * P],
-                    rhs=cq[:].bitcast(FP8X4), rhs_scale=cs[:],
-                    start=True, stop=True,
-                )
-            for k in range(2):
-                a = 2 * h + k
-                nc.scalar.activation(
-                    out=fi[:, a, :, 4:12, 8:24], in_=acc[:, k, :].rearrange("p (n r s) -> p n r s", n=NS, s=16),
-                    func=ACT.Relu, bias=bn_t[:, 4 + a:5 + a], scale=bn_s[:, 4 + a:5 + a],
-                )
-            half = fi[:, 2 * h:2 * h + 2].rearrange("p a n r s -> p (a n) r s")
-            nc.vector.tensor_copy(out=half[:, :, 4:12, 0:8], in_=half[:, :, 4:12, 8:9].to_broadcast([P, 4, 8, 8]))
-            nc.vector.tensor_copy(out=half[:, :, 4:12, 24:32], in_=half[:, :, 4:12, 23:24].to_broadcast([P, 4, 8, 8]))
-            nc.vector.tensor_copy(out=half[:, :, 0:4, :], in_=half[:, :, 4:5, :].to_broadcast([P, 4, 4, 32]))
-            nc.vector.tensor_copy(out=half[:, :, 12:16, :], in_=half[:, :, 11:12, :].to_broadcast([P, 4, 4, 32]))
-            for k in range(2):
-                a = 2 * h + k
+                product(acc[:, k, :], "img", 2 * h + k, cq, cs)
+                img_acc[2 * h + k] = acc[:, k, :]
+
+        def img_relu(tiles):
+            fi = keep.tile([P, NS, len(tiles), 16, 32], F32, name="fi%d" % tiles[0])
+            for k, a in enumerate(tiles):
+                relu("img", a, fi[:, :, k, 4:12, 8:24], img_acc[a].rearrange("p (n r s) -> p n r s", n=NS, s=16))
+            img_out[tiles[0]] = fi
+
+        def img_pad_store(tiles):
+            fi = img_out[tiles[0]]
+            g = NS * len(tiles)
+            fv = fi[:].rearrange("p n k r s -> p (n k) r s")
+            nc.vector.tensor_copy(
+                out=fv.rearrange("p g r (j c) -> p g r j c", c=8)[:, :, 4:12, 0:4:3, :],
+                in_=fv[:, :, 4:12, 8:24:15].unsqueeze(4).to_broadcast([P, g, 8, 2, 8]),
+            )
+            nc.vector.tensor_copy(
+                out=fv.rearrange("p g (j c) s -> p g j c s", c=4)[:, :, 0:4:3, :, :],
+                in_=fv[:, :, 4:12:7, :].unsqueeze(3).to_broadcast([P, g, 2, 4, 32]),
+            )
+            for n in range(NS):
                 nc.sync.dma_start(
-                    out=out_v[:, a * P:(a + 1) * P, :].rearrange("n o s -> o n s"),
-                    in_=fi[:, a].rearrange("p n r s -> p n (r s)"),
+                    out=out_v[n, 0, :, tiles[0]:tiles[-1] + 1, :], in_=fi[:, n].rearrange("p k r s -> p k (r s)"),
                 )
+
+        HALF = HW // 2
+        w_transpose("img", 0)
+        w_copy("img", 0, nc.scalar.copy)
+        w_transpose("img", 1)
+        w_copy("img", 1, nc.scalar.copy)
+        nc.vector.tensor_tensor(
+            out=cg[:], in0=f0[:].rearrange("p (n t) c -> p n c t", n=NS),
+            in1=ex[:].rearrange("p (n t) r s -> p n (r s) t", n=NS), op=ADD,
+        )
+        w_quant("img", 0, 1)
+        nc.vector.quantize_mx(out=cq[:].bitcast(FP8X4), scales=cs[:], in_=cg[:].rearrange("p n c t -> p (n c t)"))
+        bn_tail("img")
+        w_transpose("pts", 0)
+        w_copy("pts", 0, nc.scalar.copy)
+        w_transpose("pts", 1)
+        w_copy("pts", 1, nc.scalar.copy)
+        img_products(0)
+        w_quant("img", 1, 2)
+        img_relu((0,))
+        img_relu((1,))
+        img_products(1)
+        img_relu((2, 3))
+        bn_head("pts")
+        img_pad_store((0,))
+        w_quant("pts", 0, 2)
+        img_pad_store((1,))
+        x_regroup(0, nc.scalar.copy, HALF, HW)
+        x_regroup(0, nc.vector.tensor_copy, 0, HALF)
+        img_pad_store((2, 3))
+        bn_mid("pts")
+        bn_tail("pts")
+        x_quant(0)
+        x_regroup(1, nc.scalar.copy, HALF, HW)
+        x_regroup(1, nc.vector.tensor_copy, 0, HALF)
+        accs0 = pts_products(0)
+        pts_finish(0, accs0, (0,))
+        pts_finish(0, accs0, (1,))
+        x_quant(1)
+        pts_finish(0, accs0, (2, 3))
+        accs1 = pts_products(1)
+        pts_finish(1, accs1, (0, 1))
+        pts_finish(1, accs1, (2, 3))

@@ -82,10 +82,10 @@ def tile_prefusioncat_kernel(
             load_par(nc.sync, "pts", q)
         load_x(1)
 
-        one = keep.tile([P, 1], F32, name="one")
-        nc.vector.memset(one[:], 1.0)
+        eps = keep.tile([P, 1], F32, name="eps")
+        nc.vector.memset(eps[:], BN_EPS)
         warm = keep.tile([P, 1], F32, name="warm")
-        nc.scalar.activation(out=warm[:], in_=one[:], func=ACT.Sqrt)
+        nc.scalar.activation(out=warm[:], in_=eps[:], func=ACT.Sqrt)
 
         bn = {}
 
@@ -94,18 +94,17 @@ def tile_prefusioncat_kernel(
             return bn[(br, nm)]
 
         def bn_head(br):
-            nc.vector.tensor_scalar_add(out=bn_tile(br, "ve")[:], in0=par[br][:, 0, 0:OT], scalar1=BN_EPS)
-            nc.scalar.activation(out=bn_tile(br, "sd")[:], in_=bn[(br, "ve")][:], func=ACT.Sqrt)
+            nc.scalar.activation(out=bn_tile(br, "sd")[:], in_=par[br][:, 0, 0:OT], func=ACT.Sqrt, bias=eps[:], scale=1.0)
+            nc.gpsimd.tensor_tensor(out=bn_tile(br, "dm")[:], in0=par[br][:, 2, 0:OT], in1=par[br][:, 3, 0:OT], op=SUB)
 
         def bn_mid(br):
             nc.vector.reciprocal(out=bn_tile(br, "rs")[:], in_=bn[(br, "sd")][:])
 
         def bn_tail(br):
             pv = par[br]
-            nc.vector.tensor_tensor(out=bn_tile(br, "s")[:], in0=pv[:, 1, 0:OT], in1=bn[(br, "rs")][:], op=MUL)
-            nc.vector.tensor_tensor(out=bn_tile(br, "dm")[:], in0=pv[:, 2, 0:OT], in1=pv[:, 3, 0:OT], op=SUB)
-            nc.vector.tensor_tensor(out=bn_tile(br, "ds")[:], in0=bn[(br, "dm")][:], in1=bn[(br, "s")][:], op=MUL)
-            nc.vector.tensor_tensor(out=bn_tile(br, "t")[:], in0=bn[(br, "ds")][:], in1=pv[:, 4, 0:OT], op=ADD)
+            nc.gpsimd.tensor_tensor(out=bn_tile(br, "s")[:], in0=pv[:, 1, 0:OT], in1=bn[(br, "rs")][:], op=MUL)
+            nc.gpsimd.tensor_tensor(out=bn_tile(br, "ds")[:], in0=bn[(br, "dm")][:], in1=bn[(br, "s")][:], op=MUL)
+            nc.gpsimd.tensor_tensor(out=bn_tile(br, "t")[:], in0=bn[(br, "ds")][:], in1=pv[:, 4, 0:OT], op=ADD)
 
         bn_head("img")
         f0, f1, f2, f3, f4 = f_raw
@@ -120,6 +119,7 @@ def tile_prefusioncat_kernel(
             in1=g3x[:].rearrange("p q b e -> p q (b e)").unsqueeze(2).to_broadcast([P, 8, 2, 4]), op=ADD,
         )
         bn_mid("img")
+        bn_tail("img")
         g1 = keep.tile([P, 8, 4, 8], F32, name="g1")
         g1v = g1[:].rearrange("p q (a e) b -> p (q a) e b", e=2)
         f1v = f1[:].rearrange("p q (a e b) -> p (q a) e b", e=2, b=8)
@@ -144,10 +144,12 @@ def tile_prefusioncat_kernel(
             out=ex0.rearrange("p t r (j c) -> p t r j c", c=4)[:, :, 2:6, 0:4:3, :],
             in_=g10[:, :, :, 0:8:7].unsqueeze(4).to_broadcast([P, 4, 4, 2, 4]),
         )
-        nc.vector.tensor_copy(
-            out=ex[:, 4:8].rearrange("p t (a e) (b d) -> p (t a) e b d", e=2, d=2),
-            in_=g1[:, 4:8].rearrange("p t a b -> p (t a) b").unsqueeze(2).unsqueeze(4).to_broadcast([P, 16, 2, 8, 2]),
-        )
+        ex1 = ex[:, 4:8].rearrange("p t (a e) (b d) -> p (t a) e b d", e=2, d=2)
+        for e in range(2):
+            nc.scalar.copy(
+                out=ex1[:, :, e],
+                in_=g1[:, 4:8].rearrange("p t a b -> p (t a) b").unsqueeze(3).to_broadcast([P, 16, 8, 2]),
+            )
         nc.vector.tensor_copy(
             out=ex0.rearrange("p t (j c) s -> p t j c s", c=2)[:, :, 0:4:3, :, :],
             in_=ex0[:, :, 2:6:3, :].unsqueeze(3).to_broadcast([P, 4, 2, 2, 16]),
@@ -275,7 +277,6 @@ def tile_prefusioncat_kernel(
         )
         w_quant("img", 0, 1)
         nc.vector.quantize_mx(out=cq[:].bitcast(FP8X4), scales=cs[:], in_=cg[:].rearrange("p n c t -> p (n c t)"))
-        bn_tail("img")
         w_transpose("pts", 0)
         w_copy("pts", 0, nc.scalar.copy)
         w_transpose("pts", 1)
@@ -290,14 +291,13 @@ def tile_prefusioncat_kernel(
         img_pad_store((0,))
         w_quant("pts", 0, 2)
         img_pad_store((1,))
+        x_regroup(0, nc.scalar.copy, 0, HALF)
         x_regroup(0, nc.scalar.copy, HALF, HW)
-        x_regroup(0, nc.vector.tensor_copy, 0, HALF)
         img_pad_store((2, 3))
         bn_mid("pts")
         bn_tail("pts")
+        x_regroup(1, nc.vector.tensor_copy, 0, HW)
         x_quant(0)
-        x_regroup(1, nc.scalar.copy, HALF, HW)
-        x_regroup(1, nc.vector.tensor_copy, 0, HALF)
         accs0 = pts_products(0)
         pts_finish(0, accs0, (0,))
         pts_finish(0, accs0, (1,))

@@ -65,22 +65,22 @@ def tile_prefusioncat_kernel(
         def load_x(n):
             nc.sync.dma_start(out=x_raw[n][:], in_=pts_feat0[n].rearrange("(p t) h w -> p t (h w)", t=4))
 
-        img_w_v = img_w.rearrange("(p a) c -> p a c", a=OT)
+        pts_w_v = pts_w.rearrange("(p a) c -> p a c", a=OT)
         load_feat(nc.sync, 4)
         load_feat(nc.scalar, 2)
         load_feat(nc.sync, 3)
         load_feat(nc.scalar, 1)
-        load_par(nc.scalar, "img", 0)
-        load_feat(nc.sync, 0)
-        nc.sync.dma_start(out=w_raw["img"][:, 0:2, :], in_=img_w_v[:, 0:2, :])
-        nc.sync.dma_start(out=w_raw["img"][:, 2:4, :], in_=img_w_v[:, 2:4, :])
-        for q in range(1, 5):
-            load_par(nc.sync, "img", q)
-        nc.sync.dma_start(out=w_raw["pts"][:], in_=pts_w.rearrange("(p a) c -> p a c", a=OT))
+        load_par(nc.scalar, "pts", 0)
+        nc.sync.dma_start(out=w_raw["pts"][:, 0:2, :], in_=pts_w_v[:, 0:2, :])
         load_x(0)
-        for q in range(5):
+        nc.sync.dma_start(out=w_raw["pts"][:, 2:4, :], in_=pts_w_v[:, 2:4, :])
+        for q in range(1, 5):
             load_par(nc.sync, "pts", q)
+        nc.sync.dma_start(out=w_raw["img"][:], in_=img_w.rearrange("(p a) c -> p a c", a=OT))
         load_x(1)
+        load_feat(nc.sync, 0)
+        for q in range(5):
+            load_par(nc.sync, "img", q)
 
         eps = keep.tile([P, 1], F32, name="eps")
         nc.vector.memset(eps[:], BN_EPS)
@@ -106,7 +106,7 @@ def tile_prefusioncat_kernel(
             nc.gpsimd.tensor_tensor(out=bn_tile(br, "ds")[:], in0=bn[(br, "dm")][:], in1=bn[(br, "s")][:], op=MUL)
             nc.gpsimd.tensor_tensor(out=bn_tile(br, "t")[:], in0=bn[(br, "ds")][:], in1=pv[:, 4, 0:OT], op=ADD)
 
-        bn_head("img")
+        bn_head("pts")
         f0, f1, f2, f3, f4 = f_raw
         g3x = keep.tile([P, 8, 2, 2], F32, name="g3x")
         nc.vector.tensor_tensor(
@@ -118,8 +118,8 @@ def tile_prefusioncat_kernel(
             out=g2[:], in0=f2[:].rearrange("p q (a b) -> p q a b", a=2),
             in1=g3x[:].rearrange("p q b e -> p q (b e)").unsqueeze(2).to_broadcast([P, 8, 2, 4]), op=ADD,
         )
-        bn_mid("img")
-        bn_tail("img")
+        bn_mid("pts")
+        bn_tail("pts")
         g1 = keep.tile([P, 8, 4, 8], F32, name="g1")
         g1v = g1[:].rearrange("p q (a e) b -> p (q a) e b", e=2)
         f1v = f1[:].rearrange("p q (a e b) -> p (q a) e b", e=2, b=8)
@@ -139,21 +139,25 @@ def tile_prefusioncat_kernel(
         ex = keep.tile([P, 8, 8, 16], F32, name="ex")
         ex0 = ex[:, 0:4]
         g10 = g1[:, 0:4]
-        nc.vector.tensor_copy(out=ex0[:, :, 2:6, 4:12], in_=g10)
-        nc.vector.tensor_copy(
-            out=ex0.rearrange("p t r (j c) -> p t r j c", c=4)[:, :, 2:6, 0:4:3, :],
-            in_=g10[:, :, :, 0:8:7].unsqueeze(4).to_broadcast([P, 4, 4, 2, 4]),
-        )
-        ex1 = ex[:, 4:8].rearrange("p t (a e) (b d) -> p (t a) e b d", e=2, d=2)
-        for e in range(2):
-            nc.scalar.copy(
-                out=ex1[:, :, e],
-                in_=g1[:, 4:8].rearrange("p t a b -> p (t a) b").unsqueeze(3).to_broadcast([P, 16, 8, 2]),
+
+        def spread_sample1():
+            ex1 = ex[:, 4:8].rearrange("p t (a e) (b d) -> p (t a) e b d", e=2, d=2)
+            for e in range(2):
+                nc.scalar.copy(
+                    out=ex1[:, :, e],
+                    in_=g1[:, 4:8].rearrange("p t a b -> p (t a) b").unsqueeze(3).to_broadcast([P, 16, 8, 2]),
+                )
+
+        def spread_sample0():
+            nc.vector.tensor_copy(out=ex0[:, :, 2:6, 4:12], in_=g10)
+            nc.vector.tensor_copy(
+                out=ex0.rearrange("p t r (j c) -> p t r j c", c=4)[:, :, 2:6, 0:4:3, :],
+                in_=g10[:, :, :, 0:8:7].unsqueeze(4).to_broadcast([P, 4, 4, 2, 4]),
             )
-        nc.vector.tensor_copy(
-            out=ex0.rearrange("p t (j c) s -> p t j c s", c=2)[:, :, 0:4:3, :, :],
-            in_=ex0[:, :, 2:6:3, :].unsqueeze(3).to_broadcast([P, 4, 2, 2, 16]),
-        )
+            nc.vector.tensor_copy(
+                out=ex0.rearrange("p t (j c) s -> p t j c s", c=2)[:, :, 0:4:3, :, :],
+                in_=ex0[:, :, 2:6:3, :].unsqueeze(3).to_broadcast([P, 4, 2, 2, 16]),
+            )
 
         wt_ps = {}
         wgt = {}
@@ -217,13 +221,11 @@ def tile_prefusioncat_kernel(
                 bias=bn[(br, "t")][:, a:a + 1], scale=bn[(br, "s")][:, a:a + 1],
             )
 
-        def pts_products(n):
-            accs = []
-            for a in range(OT):
+        def pts_products(n, accs, tiles):
+            for a in tiles:
                 acc = pso.tile([P, HW], F32, name="acc")
                 product(acc[:], "pts", a, xt[n][1], xt[n][2])
-                accs.append(acc)
-            return accs
+                accs[a] = acc
 
         def pts_finish(n, accs, tiles):
             y = ypool.tile([P, 2, HW], F32, name="y")
@@ -266,43 +268,46 @@ def tile_prefusioncat_kernel(
                     out=out_v[n, 0, :, tiles[0]:tiles[-1] + 1, :], in_=fi[:, n].rearrange("p k r s -> p k (r s)"),
                 )
 
-        HALF = HW // 2
+        accs0 = {}
+        accs1 = {}
+        w_transpose("pts", 0)
+        w_copy("pts", 0, nc.scalar.copy)
+        spread_sample1()
+        x_regroup(0, nc.vector.tensor_copy, 0, HW)
+        w_quant("pts", 0, 1)
+        x_quant(0)
+        w_transpose("pts", 1)
+        w_copy("pts", 1, nc.scalar.copy)
         w_transpose("img", 0)
         w_copy("img", 0, nc.scalar.copy)
+        pts_products(0, accs0, (0, 1))
+        spread_sample0()
+        w_quant("pts", 1, 2)
         w_transpose("img", 1)
+        pts_products(0, accs0, (2, 3))
+        pts_finish(0, accs0, (0,))
+        pts_finish(0, accs0, (1,))
+        pts_finish(0, accs0, (2, 3))
+        x_regroup(1, nc.vector.tensor_copy, 0, HW)
+        bn_head("img")
         w_copy("img", 1, nc.scalar.copy)
+        x_quant(1)
+        bn_mid("img")
+        bn_tail("img")
+        pts_products(1, accs1, (0, 1, 2, 3))
         nc.vector.tensor_tensor(
             out=cg[:], in0=f0[:].rearrange("p (n t) c -> p n c t", n=NS),
             in1=ex[:].rearrange("p (n t) r s -> p n (r s) t", n=NS), op=ADD,
         )
-        w_quant("img", 0, 1)
+        w_quant("img", 0, 2)
         nc.vector.quantize_mx(out=cq[:].bitcast(FP8X4), scales=cs[:], in_=cg[:].rearrange("p n c t -> p (n c t)"))
-        w_transpose("pts", 0)
-        w_copy("pts", 0, nc.scalar.copy)
-        w_transpose("pts", 1)
-        w_copy("pts", 1, nc.scalar.copy)
-        img_products(0)
-        w_quant("img", 1, 2)
-        img_relu((0,))
-        img_relu((1,))
-        img_products(1)
-        img_relu((2, 3))
-        bn_head("pts")
-        img_pad_store((0,))
-        w_quant("pts", 0, 2)
-        img_pad_store((1,))
-        x_regroup(0, nc.scalar.copy, 0, HALF)
-        x_regroup(0, nc.scalar.copy, HALF, HW)
-        img_pad_store((2, 3))
-        bn_mid("pts")
-        bn_tail("pts")
-        x_regroup(1, nc.vector.tensor_copy, 0, HW)
-        x_quant(0)
-        accs0 = pts_products(0)
-        pts_finish(0, accs0, (0,))
-        pts_finish(0, accs0, (1,))
-        x_quant(1)
-        pts_finish(0, accs0, (2, 3))
-        accs1 = pts_products(1)
         pts_finish(1, accs1, (0, 1))
         pts_finish(1, accs1, (2, 3))
+        img_products(0)
+        img_products(1)
+        img_relu((0,))
+        img_pad_store((0,))
+        img_relu((1,))
+        img_pad_store((1,))
+        img_relu((2, 3))
+        img_pad_store((2, 3))

@@ -66,20 +66,21 @@ def tile_prefusioncat_kernel(
             nc.sync.dma_start(out=x_raw[n][:], in_=pts_feat0[n].rearrange("(p t) h w -> p t (h w)", t=4))
 
         pts_w_v = pts_w.rearrange("(p a) c -> p a c", a=OT)
-        load_feat(nc.sync, 4)
-        load_feat(nc.scalar, 2)
-        load_feat(nc.sync, 3)
-        load_feat(nc.scalar, 1)
-        load_par(nc.scalar, "pts", 0)
+        load_par(nc.sync, "pts", 0)
+        load_par(nc.scalar, "pts", 1)
+        load_par(nc.sync, "pts", 2)
+        load_par(nc.scalar, "pts", 3)
+        load_par(nc.scalar, "pts", 4)
         nc.sync.dma_start(out=w_raw["pts"][:, 0:2, :], in_=pts_w_v[:, 0:2, :])
         load_x(0)
         nc.sync.dma_start(out=w_raw["pts"][:, 2:4, :], in_=pts_w_v[:, 2:4, :])
-        for q in range(1, 5):
-            load_par(nc.sync, "pts", q)
+        for lvl in (4, 3, 2, 1):
+            load_feat(nc.sync, lvl)
+        load_par(nc.sync, "img", 0)
         nc.sync.dma_start(out=w_raw["img"][:], in_=img_w.rearrange("(p a) c -> p a c", a=OT))
         load_x(1)
         load_feat(nc.sync, 0)
-        for q in range(5):
+        for q in range(1, 5):
             load_par(nc.sync, "img", q)
 
         eps = keep.tile([P, 1], F32, name="eps")
@@ -95,44 +96,44 @@ def tile_prefusioncat_kernel(
 
         def bn_head(br):
             nc.scalar.activation(out=bn_tile(br, "sd")[:], in_=par[br][:, 0, 0:OT], func=ACT.Sqrt, bias=eps[:], scale=1.0)
-            nc.gpsimd.tensor_tensor(out=bn_tile(br, "dm")[:], in0=par[br][:, 2, 0:OT], in1=par[br][:, 3, 0:OT], op=SUB)
 
         def bn_mid(br):
             nc.vector.reciprocal(out=bn_tile(br, "rs")[:], in_=bn[(br, "sd")][:])
 
-        def bn_tail(br):
+        def bn_tail(br, eng):
             pv = par[br]
-            nc.gpsimd.tensor_tensor(out=bn_tile(br, "s")[:], in0=pv[:, 1, 0:OT], in1=bn[(br, "rs")][:], op=MUL)
-            nc.gpsimd.tensor_tensor(out=bn_tile(br, "ds")[:], in0=bn[(br, "dm")][:], in1=bn[(br, "s")][:], op=MUL)
-            nc.gpsimd.tensor_tensor(out=bn_tile(br, "t")[:], in0=bn[(br, "ds")][:], in1=pv[:, 4, 0:OT], op=ADD)
+            eng.tensor_tensor(out=bn_tile(br, "dm")[:], in0=pv[:, 2, 0:OT], in1=pv[:, 3, 0:OT], op=SUB)
+            eng.tensor_tensor(out=bn_tile(br, "s")[:], in0=pv[:, 1, 0:OT], in1=bn[(br, "rs")][:], op=MUL)
+            eng.tensor_tensor(out=bn_tile(br, "ds")[:], in0=bn[(br, "dm")][:], in1=bn[(br, "s")][:], op=MUL)
+            eng.tensor_tensor(out=bn_tile(br, "t")[:], in0=bn[(br, "ds")][:], in1=pv[:, 4, 0:OT], op=ADD)
 
         bn_head("pts")
+        bn_mid("pts")
+        bn_tail("pts", nc.vector)
         f0, f1, f2, f3, f4 = f_raw
         g3x = keep.tile([P, 8, 2, 2], F32, name="g3x")
-        nc.vector.tensor_tensor(
+        nc.gpsimd.tensor_tensor(
             out=g3x[:], in0=f3[:].unsqueeze(3).to_broadcast([P, 8, 2, 2]),
             in1=f4[:].unsqueeze(3).to_broadcast([P, 8, 2, 2]), op=ADD,
         )
         g2 = keep.tile([P, 8, 2, 4], F32, name="g2")
-        nc.vector.tensor_tensor(
+        nc.gpsimd.tensor_tensor(
             out=g2[:], in0=f2[:].rearrange("p q (a b) -> p q a b", a=2),
             in1=g3x[:].rearrange("p q b e -> p q (b e)").unsqueeze(2).to_broadcast([P, 8, 2, 4]), op=ADD,
         )
-        bn_mid("pts")
-        bn_tail("pts")
         g1 = keep.tile([P, 8, 4, 8], F32, name="g1")
         g1v = g1[:].rearrange("p q (a e) b -> p (q a) e b", e=2)
         f1v = f1[:].rearrange("p q (a e b) -> p (q a) e b", e=2, b=8)
         g2v = g2[:].rearrange("p q a b -> p (q a) b")
-        nc.vector.tensor_tensor(
+        nc.gpsimd.tensor_tensor(
             out=g1v[:, :, :, 2:6], in0=f1v[:, :, :, 2:6],
             in1=g2v.unsqueeze(2).to_broadcast([P, 16, 2, 4]), op=ADD,
         )
-        nc.vector.tensor_tensor(
+        nc.gpsimd.tensor_tensor(
             out=g1v[:, :, :, 0:2], in0=f1v[:, :, :, 0:2],
             in1=g2v[:, :, 0:1].unsqueeze(2).to_broadcast([P, 16, 2, 2]), op=ADD,
         )
-        nc.vector.tensor_tensor(
+        nc.gpsimd.tensor_tensor(
             out=g1v[:, :, :, 6:8], in0=f1v[:, :, :, 6:8],
             in1=g2v[:, :, 3:4].unsqueeze(2).to_broadcast([P, 16, 2, 2]), op=ADD,
         )
@@ -140,24 +141,20 @@ def tile_prefusioncat_kernel(
         ex0 = ex[:, 0:4]
         g10 = g1[:, 0:4]
 
+        def pool_copy(dst, src):
+            nc.gpsimd.tensor_scalar(out=dst, in0=src, scalar1=1.0, scalar2=0.0, op0=MUL, op1=ADD)
+
         def spread_sample1():
             ex1 = ex[:, 4:8].rearrange("p t (a e) (b d) -> p (t a) e b d", e=2, d=2)
             for e in range(2):
-                nc.scalar.copy(
-                    out=ex1[:, :, e],
-                    in_=g1[:, 4:8].rearrange("p t a b -> p (t a) b").unsqueeze(3).to_broadcast([P, 16, 8, 2]),
-                )
+                pool_copy(ex1[:, :, e], g1[:, 4:8].rearrange("p t a b -> p (t a) b").unsqueeze(3).to_broadcast([P, 16, 8, 2]))
 
         def spread_sample0():
-            nc.vector.tensor_copy(out=ex0[:, :, 2:6, 4:12], in_=g10)
-            nc.vector.tensor_copy(
-                out=ex0.rearrange("p t r (j c) -> p t r j c", c=4)[:, :, 2:6, 0:4:3, :],
-                in_=g10[:, :, :, 0:8:7].unsqueeze(4).to_broadcast([P, 4, 4, 2, 4]),
-            )
-            nc.vector.tensor_copy(
-                out=ex0.rearrange("p t (j c) s -> p t j c s", c=2)[:, :, 0:4:3, :, :],
-                in_=ex0[:, :, 2:6:3, :].unsqueeze(3).to_broadcast([P, 4, 2, 2, 16]),
-            )
+            pool_copy(ex0[:, :, 2:6, 4:12], g10)
+            pool_copy(ex0[:, :, 2:6, 0:4], g10[:, :, :, 0:1].to_broadcast([P, 4, 4, 4]))
+            pool_copy(ex0[:, :, 2:6, 12:16], g10[:, :, :, 7:8].to_broadcast([P, 4, 4, 4]))
+            pool_copy(ex0[:, :, 0:2, :], ex0[:, :, 2:3, :].to_broadcast([P, 4, 2, 16]))
+            pool_copy(ex0[:, :, 6:8, :], ex0[:, :, 5:6, :].to_broadcast([P, 4, 2, 16]))
 
         wt_ps = {}
         wgt = {}
@@ -270,18 +267,19 @@ def tile_prefusioncat_kernel(
 
         accs0 = {}
         accs1 = {}
+        spread_sample0()
+        spread_sample1()
         w_transpose("pts", 0)
         w_copy("pts", 0, nc.scalar.copy)
-        spread_sample1()
         x_regroup(0, nc.vector.tensor_copy, 0, HW)
         w_quant("pts", 0, 1)
         x_quant(0)
         w_transpose("pts", 1)
         w_copy("pts", 1, nc.scalar.copy)
         w_transpose("img", 0)
+        bn_head("img")
         w_copy("img", 0, nc.scalar.copy)
         pts_products(0, accs0, (0, 1))
-        spread_sample0()
         w_quant("pts", 1, 2)
         w_transpose("img", 1)
         pts_products(0, accs0, (2, 3))
@@ -289,11 +287,10 @@ def tile_prefusioncat_kernel(
         pts_finish(0, accs0, (1,))
         pts_finish(0, accs0, (2, 3))
         x_regroup(1, nc.vector.tensor_copy, 0, HW)
-        bn_head("img")
-        w_copy("img", 1, nc.scalar.copy)
-        x_quant(1)
         bn_mid("img")
-        bn_tail("img")
+        bn_tail("img", nc.gpsimd)
+        x_quant(1)
+        w_copy("img", 1, nc.vector.tensor_copy)
         pts_products(1, accs1, (0, 1, 2, 3))
         nc.vector.tensor_tensor(
             out=cg[:], in0=f0[:].rearrange("p (n t) c -> p n c t", n=NS),

@@ -66,16 +66,16 @@ def tile_prefusioncat_kernel(
             nc.sync.dma_start(out=x_raw[n][:], in_=pts_feat0[n].rearrange("(p t) h w -> p t (h w)", t=4))
 
         pts_w_v = pts_w.rearrange("(p a) c -> p a c", a=OT)
-        load_par(nc.sync, "pts", 0)
-        load_par(nc.scalar, "pts", 1)
-        load_par(nc.sync, "pts", 2)
-        load_par(nc.scalar, "pts", 3)
-        load_par(nc.scalar, "pts", 4)
+        load_feat(nc.sync, 4)
+        load_feat(nc.scalar, 2)
+        load_feat(nc.sync, 3)
+        load_feat(nc.scalar, 1)
+        load_par(nc.scalar, "pts", 0)
         nc.sync.dma_start(out=w_raw["pts"][:, 0:2, :], in_=pts_w_v[:, 0:2, :])
         load_x(0)
         nc.sync.dma_start(out=w_raw["pts"][:, 2:4, :], in_=pts_w_v[:, 2:4, :])
-        for lvl in (4, 3, 2, 1):
-            load_feat(nc.sync, lvl)
+        for q in range(1, 5):
+            load_par(nc.sync, "pts", q)
         load_par(nc.sync, "img", 0)
         nc.sync.dma_start(out=w_raw["img"][:], in_=img_w.rearrange("(p a) c -> p a c", a=OT))
         load_x(1)
@@ -100,40 +100,39 @@ def tile_prefusioncat_kernel(
         def bn_mid(br):
             nc.vector.reciprocal(out=bn_tile(br, "rs")[:], in_=bn[(br, "sd")][:])
 
-        def bn_tail(br, eng):
+        def bn_tail(br):
             pv = par[br]
-            eng.tensor_tensor(out=bn_tile(br, "dm")[:], in0=pv[:, 2, 0:OT], in1=pv[:, 3, 0:OT], op=SUB)
-            eng.tensor_tensor(out=bn_tile(br, "s")[:], in0=pv[:, 1, 0:OT], in1=bn[(br, "rs")][:], op=MUL)
-            eng.tensor_tensor(out=bn_tile(br, "ds")[:], in0=bn[(br, "dm")][:], in1=bn[(br, "s")][:], op=MUL)
-            eng.tensor_tensor(out=bn_tile(br, "t")[:], in0=bn[(br, "ds")][:], in1=pv[:, 4, 0:OT], op=ADD)
+            nc.gpsimd.tensor_tensor(out=bn_tile(br, "dm")[:], in0=pv[:, 2, 0:OT], in1=pv[:, 3, 0:OT], op=SUB)
+            nc.gpsimd.tensor_tensor(out=bn_tile(br, "s")[:], in0=pv[:, 1, 0:OT], in1=bn[(br, "rs")][:], op=MUL)
+            nc.gpsimd.tensor_tensor(out=bn_tile(br, "ds")[:], in0=bn[(br, "dm")][:], in1=bn[(br, "s")][:], op=MUL)
+            nc.gpsimd.tensor_tensor(out=bn_tile(br, "t")[:], in0=bn[(br, "ds")][:], in1=pv[:, 4, 0:OT], op=ADD)
 
         bn_head("pts")
-        bn_mid("pts")
-        bn_tail("pts", nc.vector)
         f0, f1, f2, f3, f4 = f_raw
         g3x = keep.tile([P, 8, 2, 2], F32, name="g3x")
-        nc.gpsimd.tensor_tensor(
+        nc.vector.tensor_tensor(
             out=g3x[:], in0=f3[:].unsqueeze(3).to_broadcast([P, 8, 2, 2]),
             in1=f4[:].unsqueeze(3).to_broadcast([P, 8, 2, 2]), op=ADD,
         )
         g2 = keep.tile([P, 8, 2, 4], F32, name="g2")
-        nc.gpsimd.tensor_tensor(
+        nc.vector.tensor_tensor(
             out=g2[:], in0=f2[:].rearrange("p q (a b) -> p q a b", a=2),
             in1=g3x[:].rearrange("p q b e -> p q (b e)").unsqueeze(2).to_broadcast([P, 8, 2, 4]), op=ADD,
         )
+        bn_mid("pts")
         g1 = keep.tile([P, 8, 4, 8], F32, name="g1")
         g1v = g1[:].rearrange("p q (a e) b -> p (q a) e b", e=2)
         f1v = f1[:].rearrange("p q (a e b) -> p (q a) e b", e=2, b=8)
         g2v = g2[:].rearrange("p q a b -> p (q a) b")
-        nc.gpsimd.tensor_tensor(
+        nc.vector.tensor_tensor(
             out=g1v[:, :, :, 2:6], in0=f1v[:, :, :, 2:6],
             in1=g2v.unsqueeze(2).to_broadcast([P, 16, 2, 4]), op=ADD,
         )
-        nc.gpsimd.tensor_tensor(
+        nc.vector.tensor_tensor(
             out=g1v[:, :, :, 0:2], in0=f1v[:, :, :, 0:2],
             in1=g2v[:, :, 0:1].unsqueeze(2).to_broadcast([P, 16, 2, 2]), op=ADD,
         )
-        nc.gpsimd.tensor_tensor(
+        nc.vector.tensor_tensor(
             out=g1v[:, :, :, 6:8], in0=f1v[:, :, :, 6:8],
             in1=g2v[:, :, 3:4].unsqueeze(2).to_broadcast([P, 16, 2, 2]), op=ADD,
         )
@@ -147,7 +146,10 @@ def tile_prefusioncat_kernel(
         def spread_sample1():
             ex1 = ex[:, 4:8].rearrange("p t (a e) (b d) -> p (t a) e b d", e=2, d=2)
             for e in range(2):
-                pool_copy(ex1[:, :, e], g1[:, 4:8].rearrange("p t a b -> p (t a) b").unsqueeze(3).to_broadcast([P, 16, 8, 2]))
+                nc.scalar.copy(
+                    out=ex1[:, :, e],
+                    in_=g1[:, 4:8].rearrange("p t a b -> p (t a) b").unsqueeze(3).to_broadcast([P, 16, 8, 2]),
+                )
 
         def spread_sample0():
             pool_copy(ex0[:, :, 2:6, 4:12], g10)
@@ -267,10 +269,11 @@ def tile_prefusioncat_kernel(
 
         accs0 = {}
         accs1 = {}
+        bn_tail("pts")
         spread_sample0()
-        spread_sample1()
         w_transpose("pts", 0)
         w_copy("pts", 0, nc.scalar.copy)
+        spread_sample1()
         x_regroup(0, nc.vector.tensor_copy, 0, HW)
         w_quant("pts", 0, 1)
         x_quant(0)
@@ -288,7 +291,7 @@ def tile_prefusioncat_kernel(
         pts_finish(0, accs0, (2, 3))
         x_regroup(1, nc.vector.tensor_copy, 0, HW)
         bn_mid("img")
-        bn_tail("img", nc.gpsimd)
+        bn_tail("img")
         x_quant(1)
         w_copy("img", 1, nc.vector.tensor_copy)
         pts_products(1, accs1, (0, 1, 2, 3))

@@ -279,21 +279,21 @@ def tile_prefusioncat_kernel(
         x_quant(0)
         w_transpose("pts", 1)
         w_copy("pts", 1, nc.scalar.copy)
-        w_transpose("img", 0)
-        bn_head("img")
-        w_copy("img", 0, nc.scalar.copy)
         pts_products(0, accs0, (0, 1))
         w_quant("pts", 1, 2)
-        w_transpose("img", 1)
         pts_products(0, accs0, (2, 3))
         pts_finish(0, accs0, (0,))
         pts_finish(0, accs0, (1,))
         pts_finish(0, accs0, (2, 3))
+        w_transpose("img", 0)
+        w_transpose("img", 1)
+        bn_head("img")
+        w_copy("img", 0, nc.scalar.copy)
         x_regroup(1, nc.vector.tensor_copy, 0, HW)
+        w_copy("img", 1, nc.vector.tensor_copy)
+        x_quant(1)
         bn_mid("img")
         bn_tail("img")
-        x_quant(1)
-        w_copy("img", 1, nc.vector.tensor_copy)
         pts_products(1, accs1, (0, 1, 2, 3))
         nc.vector.tensor_tensor(
             out=cg[:], in0=f0[:].rearrange("p (n t) c -> p n c t", n=NS),

@@ -37,7 +37,6 @@ def tile_prefusioncat_kernel(
         ypool = ctx.enter_context(tc.tile_pool(name="ypool", bufs=4))
         psw = ctx.enter_context(tc.psum_pool(name="psw", bufs=2))
         pso = ctx.enter_context(tc.psum_pool(name="pso", bufs=5))
-        ctx.enter_context(tc.manual_schedule())
 
         ident_f = keep.tile([P, P], F32, name="ident_f")
         make_identity(nc, ident_f[:])
@@ -279,21 +278,21 @@ def tile_prefusioncat_kernel(
         x_quant(0)
         w_transpose("pts", 1)
         w_copy("pts", 1, nc.scalar.copy)
+        w_transpose("img", 0)
+        bn_head("img")
+        w_copy("img", 0, nc.scalar.copy)
         pts_products(0, accs0, (0, 1))
         w_quant("pts", 1, 2)
+        w_transpose("img", 1)
         pts_products(0, accs0, (2, 3))
         pts_finish(0, accs0, (0,))
         pts_finish(0, accs0, (1,))
         pts_finish(0, accs0, (2, 3))
-        w_transpose("img", 0)
-        w_transpose("img", 1)
-        bn_head("img")
-        w_copy("img", 0, nc.scalar.copy)
         x_regroup(1, nc.vector.tensor_copy, 0, HW)
-        w_copy("img", 1, nc.vector.tensor_copy)
-        x_quant(1)
         bn_mid("img")
         bn_tail("img")
+        x_quant(1)
+        w_copy("img", 1, nc.vector.tensor_copy)
         pts_products(1, accs1, (0, 1, 2, 3))
         nc.vector.tensor_tensor(
             out=cg[:], in0=f0[:].rearrange("p (n t) c -> p n c t", n=NS),

@@ -139,9 +139,6 @@ def tile_prefusioncat_kernel(
         ex0 = ex[:, 0:4]
         g10 = g1[:, 0:4]
 
-        def pool_copy(dst, src):
-            nc.gpsimd.tensor_scalar(out=dst, in0=src, scalar1=1.0, scalar2=0.0, op0=MUL, op1=ADD)
-
         def spread_sample1():
             ex1 = ex[:, 4:8].rearrange("p t (a e) (b d) -> p (t a) e b d", e=2, d=2)
             for e in range(2):
@@ -151,11 +148,11 @@ def tile_prefusioncat_kernel(
                 )
 
         def spread_sample0():
-            pool_copy(ex0[:, :, 2:6, 4:12], g10)
-            pool_copy(ex0[:, :, 2:6, 0:4], g10[:, :, :, 0:1].to_broadcast([P, 4, 4, 4]))
-            pool_copy(ex0[:, :, 2:6, 12:16], g10[:, :, :, 7:8].to_broadcast([P, 4, 4, 4]))
-            pool_copy(ex0[:, :, 0:2, :], ex0[:, :, 2:3, :].to_broadcast([P, 4, 2, 16]))
-            pool_copy(ex0[:, :, 6:8, :], ex0[:, :, 5:6, :].to_broadcast([P, 4, 2, 16]))
+            nc.scalar.copy(out=ex0[:, :, 2:6, 4:12], in_=g10)
+            nc.scalar.copy(out=ex0[:, :, 2:6, 0:4], in_=g10[:, :, :, 0:1].to_broadcast([P, 4, 4, 4]))
+            nc.scalar.copy(out=ex0[:, :, 2:6, 12:16], in_=g10[:, :, :, 7:8].to_broadcast([P, 4, 4, 4]))
+            nc.scalar.copy(out=ex0[:, :, 0:2, :], in_=ex0[:, :, 2:3, :].to_broadcast([P, 4, 2, 16]))
+            nc.scalar.copy(out=ex0[:, :, 6:8, :], in_=ex0[:, :, 5:6, :].to_broadcast([P, 4, 2, 16]))
 
         wt_ps = {}
         wgt = {}

@@ -76,8 +76,10 @@ def tile_prefusioncat_kernel(
         for q in range(1, 5):
             load_par(nc.sync, "pts", q)
         load_par(nc.sync, "img", 0)
-        nc.sync.dma_start(out=w_raw["img"][:], in_=img_w.rearrange("(p a) c -> p a c", a=OT))
+        img_w_v = img_w.rearrange("(p a) c -> p a c", a=OT)
+        nc.sync.dma_start(out=w_raw["img"][:, 0:2, :], in_=img_w_v[:, 0:2, :])
         load_x(1)
+        nc.sync.dma_start(out=w_raw["img"][:, 2:4, :], in_=img_w_v[:, 2:4, :])
         load_feat(nc.sync, 0)
         for q in range(1, 5):
             load_par(nc.sync, "img", q)

@@ -36,10 +36,17 @@ def tile_prefusioncat_kernel(
         keep = ctx.enter_context(tc.tile_pool(name="keep", bufs=1))
         ypool = ctx.enter_context(tc.tile_pool(name="ypool", bufs=4))
         psw = ctx.enter_context(tc.psum_pool(name="psw", bufs=2))
+        psd = ctx.enter_context(tc.psum_pool(name="psd", bufs=1))
         pso = ctx.enter_context(tc.psum_pool(name="pso", bufs=5))
 
         ident_f = keep.tile([P, P], F32, name="ident_f")
         make_identity(nc, ident_f[:])
+
+        zeros = keep.tile([P, HW], BF16, name="zeros")
+        nc.vector.memset(zeros[:], 0.0)
+        idle_acc = psd.tile([P, HW], F32, name="idle_acc")
+        for rep in range(4):
+            nc.tensor.matmul(idle_acc[:], lhsT=zeros[:, 0:P], rhs=zeros[:], start=True, stop=True)
 
         w_raw = {"pts": keep.tile([P, OT, C], BF16, name="w_raw_pts"), "img": keep.tile([P, OT, C], BF16, name="w_raw_img")}
         x_raw = [keep.tile([P, 4, HW], BF16, name="x_raw%d" % n) for n in range(NS)]

@@ -34,19 +34,13 @@ def tile_prefusioncat_kernel(
     out_v = out.rearrange("n (b p a) h w -> n b p a (h w)", b=2, a=OT)
     with ExitStack() as ctx:
         keep = ctx.enter_context(tc.tile_pool(name="keep", bufs=1))
-        ypool = ctx.enter_context(tc.tile_pool(name="ypool", bufs=4))
-        psw = ctx.enter_context(tc.psum_pool(name="psw", bufs=2))
-        psd = ctx.enter_context(tc.psum_pool(name="psd", bufs=1))
+        ypool = ctx.enter_context(tc.tile_pool(name="ypool", bufs=8))
+        psw = ctx.enter_context(tc.psum_pool(name="psw", bufs=3))
         pso = ctx.enter_context(tc.psum_pool(name="pso", bufs=5))
 
+        ctx.enter_context(tc.manual_schedule())
         ident_f = keep.tile([P, P], F32, name="ident_f")
         make_identity(nc, ident_f[:])
-
-        zeros = keep.tile([P, HW], BF16, name="zeros")
-        nc.vector.memset(zeros[:], 0.0)
-        idle_acc = psd.tile([P, HW], F32, name="idle_acc")
-        for rep in range(4):
-            nc.tensor.matmul(idle_acc[:], lhsT=zeros[:, 0:P], rhs=zeros[:], start=True, stop=True)
 
         w_raw = {"pts": keep.tile([P, OT, C], BF16, name="w_raw_pts"), "img": keep.tile([P, OT, C], BF16, name="w_raw_img")}
         x_raw = [keep.tile([P, 4, HW], BF16, name="x_raw%d" % n) for n in range(NS)]
@@ -72,29 +66,32 @@ def tile_prefusioncat_kernel(
             nc.sync.dma_start(out=x_raw[n][:], in_=pts_feat0[n].rearrange("(p t) h w -> p t (h w)", t=4))
 
         pts_w_v = pts_w.rearrange("(p a) c -> p a c", a=OT)
+        img_w_v = img_w.rearrange("(p a) c -> p a c", a=OT)
+        w_views = {"pts": pts_w_v, "img": img_w_v}
+
+        def load_w(br, lo, hi):
+            nc.sync.dma_start(out=w_raw[br][:, lo:hi, :], in_=w_views[br][:, lo:hi, :])
+
         load_feat(nc.sync, 4)
         load_feat(nc.scalar, 2)
         load_feat(nc.sync, 3)
         load_feat(nc.scalar, 1)
         load_par(nc.scalar, "pts", 0)
-        nc.sync.dma_start(out=w_raw["pts"][:, 0:2, :], in_=pts_w_v[:, 0:2, :])
         load_x(0)
-        nc.sync.dma_start(out=w_raw["pts"][:, 2:4, :], in_=pts_w_v[:, 2:4, :])
+        load_w("pts", 0, 2)
+        load_w("pts", 2, 4)
         for q in range(1, 5):
             load_par(nc.sync, "pts", q)
-        load_par(nc.sync, "img", 0)
-        img_w_v = img_w.rearrange("(p a) c -> p a c", a=OT)
-        nc.sync.dma_start(out=w_raw["img"][:, 0:2, :], in_=img_w_v[:, 0:2, :])
         load_x(1)
-        nc.sync.dma_start(out=w_raw["img"][:, 2:4, :], in_=img_w_v[:, 2:4, :])
         load_feat(nc.sync, 0)
-        for q in range(1, 5):
+        load_w("img", 0, 2)
+        load_w("img", 2, 4)
+        for q in range(5):
             load_par(nc.sync, "img", q)
-
         eps = keep.tile([P, 1], F32, name="eps")
         nc.vector.memset(eps[:], BN_EPS)
         warm = keep.tile([P, 1], F32, name="warm")
-        nc.scalar.activation(out=warm[:], in_=eps[:], func=ACT.Sqrt)
+        nc.scalar.activation(out=warm[:], in_=eps[:], func=ACT.Abs_reciprocal_sqrt)
 
         bn = {}
 
@@ -103,19 +100,22 @@ def tile_prefusioncat_kernel(
             return bn[(br, nm)]
 
         def bn_head(br):
-            nc.scalar.activation(out=bn_tile(br, "sd")[:], in_=par[br][:, 0, 0:OT], func=ACT.Sqrt, bias=eps[:], scale=1.0)
+            nc.scalar.activation(
+                out=bn_tile(br, "rs")[:], in_=par[br][:, 0, 0:OT], func=ACT.Abs_reciprocal_sqrt, bias=eps[:], scale=1.0,
+            )
 
-        def bn_mid(br):
-            nc.vector.reciprocal(out=bn_tile(br, "rs")[:], in_=bn[(br, "sd")][:])
+        def bn_dm(br, eng):
+            eng.tensor_tensor(out=bn_tile(br, "dm")[:], in0=par[br][:, 2, 0:OT], in1=par[br][:, 3, 0:OT], op=SUB)
 
-        def bn_tail(br):
-            pv = par[br]
-            nc.gpsimd.tensor_tensor(out=bn_tile(br, "dm")[:], in0=pv[:, 2, 0:OT], in1=pv[:, 3, 0:OT], op=SUB)
-            nc.gpsimd.tensor_tensor(out=bn_tile(br, "s")[:], in0=pv[:, 1, 0:OT], in1=bn[(br, "rs")][:], op=MUL)
-            nc.gpsimd.tensor_tensor(out=bn_tile(br, "ds")[:], in0=bn[(br, "dm")][:], in1=bn[(br, "s")][:], op=MUL)
-            nc.gpsimd.tensor_tensor(out=bn_tile(br, "t")[:], in0=bn[(br, "ds")][:], in1=pv[:, 4, 0:OT], op=ADD)
+        def bn_s(br, eng):
+            eng.tensor_tensor(out=bn_tile(br, "s")[:], in0=par[br][:, 1, 0:OT], in1=bn[(br, "rs")][:], op=MUL)
 
-        bn_head("pts")
+        def bn_ds(br, eng):
+            eng.tensor_tensor(out=bn_tile(br, "ds")[:], in0=bn[(br, "dm")][:], in1=bn[(br, "s")][:], op=MUL)
+
+        def bn_t(br, eng):
+            eng.tensor_tensor(out=bn_tile(br, "t")[:], in0=bn[(br, "ds")][:], in1=par[br][:, 4, 0:OT], op=ADD)
+
         f0, f1, f2, f3, f4 = f_raw
         g3x = keep.tile([P, 8, 2, 2], F32, name="g3x")
         nc.vector.tensor_tensor(
@@ -127,7 +127,6 @@ def tile_prefusioncat_kernel(
             out=g2[:], in0=f2[:].rearrange("p q (a b) -> p q a b", a=2),
             in1=g3x[:].rearrange("p q b e -> p q (b e)").unsqueeze(2).to_broadcast([P, 8, 2, 4]), op=ADD,
         )
-        bn_mid("pts")
         g1 = keep.tile([P, 8, 4, 8], F32, name="g1")
         g1v = g1[:].rearrange("p q (a e) b -> p (q a) e b", e=2)
         f1v = f1[:].rearrange("p q (a e b) -> p (q a) e b", e=2, b=8)
@@ -144,24 +143,29 @@ def tile_prefusioncat_kernel(
             out=g1v[:, :, :, 6:8], in0=f1v[:, :, :, 6:8],
             in1=g2v[:, :, 3:4].unsqueeze(2).to_broadcast([P, 16, 2, 2]), op=ADD,
         )
-        ex = keep.tile([P, 8, 8, 16], F32, name="ex")
-        ex0 = ex[:, 0:4]
+        ex0 = keep.tile([P, 4, 8, 16], F32, name="ex0")
+        ex1 = keep.tile([P, 4, 16, 4], F32, name="ex1")
         g10 = g1[:, 0:4]
 
-        def spread_sample1():
-            ex1 = ex[:, 4:8].rearrange("p t (a e) (b d) -> p (t a) e b d", e=2, d=2)
-            for e in range(2):
-                nc.scalar.copy(
-                    out=ex1[:, :, e],
-                    in_=g1[:, 4:8].rearrange("p t a b -> p (t a) b").unsqueeze(3).to_broadcast([P, 16, 8, 2]),
-                )
+        def spread_copy(dst, src):
+            nc.gpsimd.tensor_copy(out=dst, in_=src)
 
         def spread_sample0():
-            nc.scalar.copy(out=ex0[:, :, 2:6, 4:12], in_=g10)
-            nc.scalar.copy(out=ex0[:, :, 2:6, 0:4], in_=g10[:, :, :, 0:1].to_broadcast([P, 4, 4, 4]))
-            nc.scalar.copy(out=ex0[:, :, 2:6, 12:16], in_=g10[:, :, :, 7:8].to_broadcast([P, 4, 4, 4]))
-            nc.scalar.copy(out=ex0[:, :, 0:2, :], in_=ex0[:, :, 2:3, :].to_broadcast([P, 4, 2, 16]))
-            nc.scalar.copy(out=ex0[:, :, 6:8, :], in_=ex0[:, :, 5:6, :].to_broadcast([P, 4, 2, 16]))
+            spread_copy(ex0[:, :, 2:6, 4:12], g10)
+            spread_copy(
+                ex0[:, :, 2:6, :].rearrange("p t r (j c) -> p t r j c", c=4)[:, :, :, 0:4:3, :],
+                g10[:, :, :, 0:8:7].unsqueeze(4).to_broadcast([P, 4, 4, 2, 4]),
+            )
+            spread_copy(
+                ex0[:].rearrange("p t (j r) c -> p t j r c", r=2)[:, :, 0:4:3, :, :],
+                ex0[:, :, 2:6:3, :].unsqueeze(3).to_broadcast([P, 4, 2, 2, 16]),
+            )
+
+        def spread_sample1():
+            spread_copy(
+                ex1[:].rearrange("p a (b d) t -> p a b d t", d=2),
+                g1[:, 4:8].rearrange("p t a b -> p a b t").unsqueeze(3).to_broadcast([P, 4, 8, 2, 4]),
+            )
 
         wt_ps = {}
         wgt = {}
@@ -172,23 +176,23 @@ def tile_prefusioncat_kernel(
                 keep.tile([P, O], U8, name="ws_" + br, align_bytes=64),
             )
 
-        def w_transpose(br, h):
+        def w_transpose(br, lo, hi):
             words = w_raw[br][:].bitcast(F32).rearrange("p a (m u) -> p a u m", u=2)
-            wt = psw.tile([P, 2, 2, P], F32, name="wt")
-            for a in range(2):
+            wt = psw.tile([P, hi - lo, 2, P], F32, name="wt")
+            for a in range(lo, hi):
                 for u in range(2):
-                    nc.tensor.transpose(wt[:, a, u, :], words[:, 2 * h + a, u, :], ident_f[:])
-            wt_ps[(br, h)] = wt
+                    nc.tensor.transpose(wt[:, a - lo, u, :], words[:, a, u, :], ident_f[:])
+            wt_ps[(br, lo)] = wt
 
-        def w_copy(br, h, copy_out):
+        def w_copy(br, lo, hi, copy_out):
             wg_w = wgt[br][0][:].bitcast(F32).rearrange("p (a o u) -> p a o u", a=OT, u=2)
-            copy_out(out=wg_w[:, 2 * h:2 * h + 2], in_=wt_ps[(br, h)][:].rearrange("p a u o -> p a o u"))
+            copy_out(out=wg_w[:, lo:hi], in_=wt_ps[(br, lo)][:].rearrange("p a u o -> p a o u"))
 
         def w_quant(br, lo, hi):
             wg, wq, ws = wgt[br]
             nc.vector.quantize_mx(
-                out=wq[:, lo * 256:hi * 256].bitcast(FP8X4), scales=ws[:, lo * 256:hi * 256],
-                in_=wg[:, lo * 1024:hi * 1024],
+                out=wq[:, lo * P:hi * P].bitcast(FP8X4), scales=ws[:, lo * P:hi * P],
+                in_=wg[:, lo * 4 * P:hi * 4 * P],
             )
 
         xt = [
@@ -206,16 +210,18 @@ def tile_prefusioncat_kernel(
                 in_=x_raw[n][:, :, lo:hi].rearrange("p t (c i) -> p c t i", i=4),
             )
 
-        def x_quant(n):
+        def x_quant(n, lo=0, hi=HW):
             xg, xq, xs = xt[n]
-            nc.vector.quantize_mx(out=xq[:].bitcast(FP8X4), scales=xs[:], in_=xg[:].rearrange("p c t -> p (c t)"))
+            nc.vector.quantize_mx(
+                out=xq[:, lo:hi].bitcast(FP8X4), scales=xs[:, lo:hi], in_=xg[:, lo:hi, :].rearrange("p c t -> p (c t)"),
+            )
 
         def product(acc, br, a, rq, rs_):
             wq, ws = wgt[br][1], wgt[br][2]
             nc.tensor.matmul_mx(
                 out=acc,
                 lhsT=wq[:, a * P:(a + 1) * P].bitcast(FP8X4), lhsT_scale=ws[:, a * P:(a + 1) * P],
-                rhs=rq[:].bitcast(FP8X4), rhs_scale=rs_[:],
+                rhs=rq.bitcast(FP8X4), rhs_scale=rs_,
                 start=True, stop=True,
             )
 
@@ -228,7 +234,7 @@ def tile_prefusioncat_kernel(
         def pts_products(n, accs, tiles):
             for a in tiles:
                 acc = pso.tile([P, HW], F32, name="acc")
-                product(acc[:], "pts", a, xt[n][1], xt[n][2])
+                product(acc[:], "pts", a, xt[n][1][:], xt[n][2][:])
                 accs[a] = acc
 
         def pts_finish(n, accs, tiles):
@@ -236,6 +242,22 @@ def tile_prefusioncat_kernel(
             for k, a in enumerate(tiles):
                 relu("pts", a, y[:, k, :], accs[a][:])
             nc.sync.dma_start(out=out_v[n, 1, :, tiles[0]:tiles[-1] + 1, :], in_=y[:, 0:len(tiles), :])
+
+        def half_products(h):
+            acc = pso.tile([P, 2, HW // 2], F32, name="acc")
+            cols = slice(h * HW // 2, (h + 1) * HW // 2)
+            for a in range(2):
+                product(acc[:, a, :], "pts", a, xt[0][1][:, cols], xt[0][2][:, cols])
+            half_acc[h] = acc
+
+        def half_finish(h):
+            y = ypool.tile([P, 2, HW // 2], F32, name="yh")
+            cols = slice(h * HW // 2, (h + 1) * HW // 2)
+            for a in range(2):
+                relu("pts", a, y[:, a, :], half_acc[h][:, a, :])
+            nc.sync.dma_start(out=out_v[0, 1, :, 0:2, cols], in_=y[:])
+
+        half_acc = {}
 
         cg = keep.tile([P, NS, P, 4], BF16, name="cg", align_bytes=64)
         cq = keep.tile([P, NS * P], U32, name="cq", align_bytes=64)
@@ -246,7 +268,7 @@ def tile_prefusioncat_kernel(
         def img_products(h):
             acc = pso.tile([P, 2, NS * P], F32, name="acc")
             for k in range(2):
-                product(acc[:, k, :], "img", 2 * h + k, cq, cs)
+                product(acc[:, k, :], "img", 2 * h + k, cq[:], cs[:])
                 img_acc[2 * h + k] = acc[:, k, :]
 
         def img_relu(tiles):
@@ -255,64 +277,111 @@ def tile_prefusioncat_kernel(
                 relu("img", a, fi[:, :, k, 4:12, 8:24], img_acc[a].rearrange("p (n r s) -> p n r s", n=NS, s=16))
             img_out[tiles[0]] = fi
 
-        def img_pad_store(tiles):
-            fi = img_out[tiles[0]]
-            g = NS * len(tiles)
+        def img_pad_cols(a):
+            fi = img_out[a]
+            g = fi.shape[1] * fi.shape[2]
             fv = fi[:].rearrange("p n k r s -> p (n k) r s")
             nc.vector.tensor_copy(
                 out=fv.rearrange("p g r (j c) -> p g r j c", c=8)[:, :, 4:12, 0:4:3, :],
                 in_=fv[:, :, 4:12, 8:24:15].unsqueeze(4).to_broadcast([P, g, 8, 2, 8]),
             )
+
+        def img_pad_rows(a):
+            fi = img_out[a]
+            g = fi.shape[1] * fi.shape[2]
+            fv = fi[:].rearrange("p n k r s -> p (n k) r s")
             nc.vector.tensor_copy(
                 out=fv.rearrange("p g (j c) s -> p g j c s", c=4)[:, :, 0:4:3, :, :],
                 in_=fv[:, :, 4:12:7, :].unsqueeze(3).to_broadcast([P, g, 2, 4, 32]),
             )
+
+        def img_pad(a):
+            img_pad_cols(a)
+            img_pad_rows(a)
+
+        def img_store(a):
+            fi = img_out[a]
             for n in range(NS):
                 nc.sync.dma_start(
-                    out=out_v[n, 0, :, tiles[0]:tiles[-1] + 1, :], in_=fi[:, n].rearrange("p k r s -> p k (r s)"),
+                    out=out_v[n, 0, :, a:a + fi.shape[2], :], in_=fi[:, n].rearrange("p k r s -> p k (r s)"),
                 )
+
+        def core_add():
+            nc.vector.tensor_tensor(
+                out=cg[:, 0], in0=f0[:, 0:4].rearrange("p t c -> p c t"), in1=ex0[:].rearrange("p t r s -> p (r s) t"), op=ADD,
+            )
+            nc.vector.tensor_tensor(
+                out=cg[:, 1].rearrange("p (a e m) t -> p a e m t", a=4, e=2),
+                in0=f0[:, 4:8].rearrange("p t (a e m) -> p a e m t", a=4, e=2),
+                in1=ex1[:].unsqueeze(2).to_broadcast([P, 4, 2, 16, 4]), op=ADD,
+            )
+
+        def core_quant():
+            nc.vector.quantize_mx(out=cq[:].bitcast(FP8X4), scales=cs[:], in_=cg[:].rearrange("p n c t -> p (n c t)"))
 
         accs0 = {}
         accs1 = {}
-        bn_tail("pts")
         spread_sample0()
-        w_transpose("pts", 0)
-        w_copy("pts", 0, nc.scalar.copy)
         spread_sample1()
-        x_regroup(0, nc.vector.tensor_copy, 0, HW)
+        bn_head("pts")
+        w_transpose("pts", 0, 1)
+        w_transpose("pts", 1, 2)
+        x_regroup(0, nc.vector.tensor_copy, 0, 256)
+        x_regroup(0, nc.scalar.copy, 352, HW)
+        x_regroup(0, nc.vector.tensor_copy, 256, 352)
+        w_copy("pts", 0, 1, nc.scalar.copy)
+        w_copy("pts", 1, 2, nc.scalar.copy)
+        w_transpose("pts", 2, 4)
+        w_copy("pts", 2, 4, nc.scalar.copy)
+        x_quant(0, 0, 256)
+        bn_s("pts", nc.vector)
+        bn_dm("pts", nc.vector)
+        x_quant(0, 256, HW)
+        bn_ds("pts", nc.vector)
         w_quant("pts", 0, 1)
-        x_quant(0)
-        w_transpose("pts", 1)
-        w_copy("pts", 1, nc.scalar.copy)
-        w_transpose("img", 0)
-        bn_head("img")
-        w_copy("img", 0, nc.scalar.copy)
-        pts_products(0, accs0, (0, 1))
+        bn_t("pts", nc.vector)
         w_quant("pts", 1, 2)
-        w_transpose("img", 1)
-        pts_products(0, accs0, (2, 3))
+        x_regroup(1, nc.vector.tensor_copy, 0, 256)
+        pts_products(0, accs0, (0,))
+        pts_products(0, accs0, (1,))
         pts_finish(0, accs0, (0,))
+        w_quant("pts", 2, 4)
+        x_regroup(1, nc.vector.tensor_copy, 256, HW)
+        pts_products(0, accs0, (2, 3))
         pts_finish(0, accs0, (1,))
-        pts_finish(0, accs0, (2, 3))
-        x_regroup(1, nc.vector.tensor_copy, 0, HW)
-        bn_mid("img")
-        bn_tail("img")
-        x_quant(1)
-        w_copy("img", 1, nc.vector.tensor_copy)
+        pts_finish(0, accs0, (2,))
+        pts_finish(0, accs0, (3,))
+        w_transpose("img", 0, 2)
+        x_quant(1, 0, 256)
+        x_quant(1, 256, HW)
+        core_add()
+        bn_head("img")
+        bn_dm("img", nc.gpsimd)
+        bn_s("img", nc.gpsimd)
+        bn_ds("img", nc.gpsimd)
+        bn_t("img", nc.gpsimd)
         pts_products(1, accs1, (0, 1, 2, 3))
-        nc.vector.tensor_tensor(
-            out=cg[:], in0=f0[:].rearrange("p (n t) c -> p n c t", n=NS),
-            in1=ex[:].rearrange("p (n t) r s -> p n (r s) t", n=NS), op=ADD,
-        )
+        w_copy("img", 0, 2, nc.vector.tensor_copy)
+        core_quant()
         w_quant("img", 0, 2)
-        nc.vector.quantize_mx(out=cq[:].bitcast(FP8X4), scales=cs[:], in_=cg[:].rearrange("p n c t -> p (n c t)"))
-        pts_finish(1, accs1, (0, 1))
-        pts_finish(1, accs1, (2, 3))
+        w_transpose("img", 2, 4)
+        pts_finish(1, accs1, (0,))
+        pts_finish(1, accs1, (1,))
         img_products(0)
-        img_products(1)
+        w_copy("img", 2, 4, nc.vector.tensor_copy)
+        pts_finish(1, accs1, (2,))
+        pts_finish(1, accs1, (3,))
         img_relu((0,))
-        img_pad_store((0,))
+        w_quant("img", 2, 4)
+        img_pad_cols(0)
+        img_pad_rows(0)
+        img_store(0)
         img_relu((1,))
-        img_pad_store((1,))
+        img_products(1)
+        img_pad_cols(1)
         img_relu((2, 3))
-        img_pad_store((2, 3))
+        img_pad_rows(1)
+        img_store(1)
+        img_pad_cols(2)
+        img_pad_rows(2)
+        img_store(2)

@@ -118,31 +118,31 @@ def tile_prefusioncat_kernel(
 
         f0, f1, f2, f3, f4 = f_raw
         g3x = keep.tile([P, 8, 2, 2], F32, name="g3x")
-        nc.vector.tensor_tensor(
-            out=g3x[:], in0=f3[:].unsqueeze(3).to_broadcast([P, 8, 2, 2]),
-            in1=f4[:].unsqueeze(3).to_broadcast([P, 8, 2, 2]), op=ADD,
-        )
         g2 = keep.tile([P, 8, 2, 4], F32, name="g2")
-        nc.vector.tensor_tensor(
-            out=g2[:], in0=f2[:].rearrange("p q (a b) -> p q a b", a=2),
-            in1=g3x[:].rearrange("p q b e -> p q (b e)").unsqueeze(2).to_broadcast([P, 8, 2, 4]), op=ADD,
-        )
         g1 = keep.tile([P, 8, 4, 8], F32, name="g1")
-        g1v = g1[:].rearrange("p q (a e) b -> p (q a) e b", e=2)
-        f1v = f1[:].rearrange("p q (a e b) -> p (q a) e b", e=2, b=8)
-        g2v = g2[:].rearrange("p q a b -> p (q a) b")
-        nc.vector.tensor_tensor(
-            out=g1v[:, :, :, 2:6], in0=f1v[:, :, :, 2:6],
-            in1=g2v.unsqueeze(2).to_broadcast([P, 16, 2, 4]), op=ADD,
-        )
-        nc.vector.tensor_tensor(
-            out=g1v[:, :, :, 0:2], in0=f1v[:, :, :, 0:2],
-            in1=g2v[:, :, 0:1].unsqueeze(2).to_broadcast([P, 16, 2, 2]), op=ADD,
-        )
-        nc.vector.tensor_tensor(
-            out=g1v[:, :, :, 6:8], in0=f1v[:, :, :, 6:8],
-            in1=g2v[:, :, 3:4].unsqueeze(2).to_broadcast([P, 16, 2, 2]), op=ADD,
-        )
+
+        def pyramid_34():
+            nc.vector.tensor_tensor(
+                out=g3x[:], in0=f3[:].unsqueeze(3).to_broadcast([P, 8, 2, 2]),
+                in1=f4[:].unsqueeze(3).to_broadcast([P, 8, 2, 2]), op=ADD,
+            )
+
+        def pyramid_2():
+            nc.vector.tensor_tensor(
+                out=g2[:], in0=f2[:].rearrange("p q (a b) -> p q a b", a=2),
+                in1=g3x[:].rearrange("p q b e -> p q (b e)").unsqueeze(2).to_broadcast([P, 8, 2, 4]), op=ADD,
+            )
+
+        def pyramid_1():
+            g1v = g1[:].rearrange("p q (a e) b -> p (q a) e b", e=2)
+            f1v = f1[:].rearrange("p q (a e b) -> p (q a) e b", e=2, b=8)
+            g2v = g2[:].rearrange("p q a b -> p (q a) b")
+            for lo, hi, src in ((2, 6, slice(0, 4)), (0, 2, slice(0, 1)), (6, 8, slice(3, 4))):
+                nc.vector.tensor_tensor(
+                    out=g1v[:, :, :, lo:hi], in0=f1v[:, :, :, lo:hi],
+                    in1=g2v[:, :, src].unsqueeze(2).to_broadcast([P, 16, 2, hi - lo]), op=ADD,
+                )
+
         ex0 = keep.tile([P, 4, 8, 16], F32, name="ex0")
         ex1 = keep.tile([P, 4, 16, 4], F32, name="ex1")
         g10 = g1[:, 0:4]
@@ -150,12 +150,14 @@ def tile_prefusioncat_kernel(
         def spread_copy(dst, src):
             nc.gpsimd.tensor_copy(out=dst, in_=src)
 
-        def spread_sample0():
+        def spread_cols0():
             spread_copy(ex0[:, :, 2:6, 4:12], g10)
             spread_copy(
                 ex0[:, :, 2:6, :].rearrange("p t r (j c) -> p t r j c", c=4)[:, :, :, 0:4:3, :],
                 g10[:, :, :, 0:8:7].unsqueeze(4).to_broadcast([P, 4, 4, 2, 4]),
             )
+
+        def spread_rows0():
             spread_copy(
                 ex0[:].rearrange("p t (j r) c -> p t j r c", r=2)[:, :, 0:4:3, :, :],
                 ex0[:, :, 2:6:3, :].unsqueeze(3).to_broadcast([P, 4, 2, 2, 16]),
@@ -271,25 +273,30 @@ def tile_prefusioncat_kernel(
                 product(acc[:, k, :], "img", 2 * h + k, cq[:], cs[:])
                 img_acc[2 * h + k] = acc[:, k, :]
 
-        def img_relu(tiles):
-            fi = keep.tile([P, NS, len(tiles), 16, 32], F32, name="fi%d" % tiles[0])
+        def img_relu(tiles, samples=(0, 1)):
+            if tiles[0] not in img_out:
+                img_out[tiles[0]] = keep.tile([P, NS, len(tiles), 16, 32], F32, name="fi%d" % tiles[0])
+            fi = img_out[tiles[0]]
+            lo, hi = samples[0], samples[-1] + 1
             for k, a in enumerate(tiles):
-                relu("img", a, fi[:, :, k, 4:12, 8:24], img_acc[a].rearrange("p (n r s) -> p n r s", n=NS, s=16))
-            img_out[tiles[0]] = fi
+                relu(
+                    "img", a, fi[:, lo:hi, k, 4:12, 8:24],
+                    img_acc[a].rearrange("p (n r s) -> p n r s", n=NS, s=16)[:, lo:hi],
+                )
 
-        def img_pad_cols(a):
+        def img_pad_cols(a, lo=0, hi=NS):
             fi = img_out[a]
-            g = fi.shape[1] * fi.shape[2]
-            fv = fi[:].rearrange("p n k r s -> p (n k) r s")
+            g = (hi - lo) * fi.shape[2]
+            fv = fi[:, lo:hi].rearrange("p n k r s -> p (n k) r s")
             nc.vector.tensor_copy(
                 out=fv.rearrange("p g r (j c) -> p g r j c", c=8)[:, :, 4:12, 0:4:3, :],
                 in_=fv[:, :, 4:12, 8:24:15].unsqueeze(4).to_broadcast([P, g, 8, 2, 8]),
             )
 
-        def img_pad_rows(a):
+        def img_pad_rows(a, lo=0, hi=NS):
             fi = img_out[a]
-            g = fi.shape[1] * fi.shape[2]
-            fv = fi[:].rearrange("p n k r s -> p (n k) r s")
+            g = (hi - lo) * fi.shape[2]
+            fv = fi[:, lo:hi].rearrange("p n k r s -> p (n k) r s")
             nc.vector.tensor_copy(
                 out=fv.rearrange("p g (j c) s -> p g j c s", c=4)[:, :, 0:4:3, :, :],
                 in_=fv[:, :, 4:12:7, :].unsqueeze(3).to_broadcast([P, g, 2, 4, 32]),
@@ -299,9 +306,9 @@ def tile_prefusioncat_kernel(
             img_pad_cols(a)
             img_pad_rows(a)
 
-        def img_store(a):
+        def img_store(a, lo=0, hi=NS):
             fi = img_out[a]
-            for n in range(NS):
+            for n in range(lo, hi):
                 nc.sync.dma_start(
                     out=out_v[n, 0, :, a:a + fi.shape[2], :], in_=fi[:, n].rearrange("p k r s -> p k (r s)"),
                 )
@@ -321,31 +328,39 @@ def tile_prefusioncat_kernel(
 
         accs0 = {}
         accs1 = {}
-        spread_sample0()
-        spread_sample1()
+        pyramid_34()
+        pyramid_2()
+        pyramid_1()
+
+        spread_cols0()
         bn_head("pts")
+        bn_s("pts", nc.gpsimd)
+        bn_dm("pts", nc.gpsimd)
+        bn_ds("pts", nc.gpsimd)
+        bn_t("pts", nc.gpsimd)
+        spread_rows0()
+        spread_sample1()
         w_transpose("pts", 0, 1)
         w_transpose("pts", 1, 2)
         x_regroup(0, nc.vector.tensor_copy, 0, 256)
-        x_regroup(0, nc.scalar.copy, 352, HW)
-        x_regroup(0, nc.vector.tensor_copy, 256, 352)
+        x_regroup(0, nc.scalar.copy, 320, HW)
+        x_regroup(0, nc.vector.tensor_copy, 256, 320)
         w_copy("pts", 0, 1, nc.scalar.copy)
         w_copy("pts", 1, 2, nc.scalar.copy)
-        w_transpose("pts", 2, 4)
-        w_copy("pts", 2, 4, nc.scalar.copy)
+        w_transpose("pts", 2, 3)
+        w_copy("pts", 2, 3, nc.scalar.copy)
+        w_transpose("pts", 3, 4)
+        w_copy("pts", 3, 4, nc.scalar.copy)
         x_quant(0, 0, 256)
-        bn_s("pts", nc.vector)
-        bn_dm("pts", nc.vector)
         x_quant(0, 256, HW)
-        bn_ds("pts", nc.vector)
         w_quant("pts", 0, 1)
-        bn_t("pts", nc.vector)
         w_quant("pts", 1, 2)
+        w_quant("pts", 2, 3)
         x_regroup(1, nc.vector.tensor_copy, 0, 256)
         pts_products(0, accs0, (0,))
         pts_products(0, accs0, (1,))
         pts_finish(0, accs0, (0,))
-        w_quant("pts", 2, 4)
+        w_quant("pts", 3, 4)
         x_regroup(1, nc.vector.tensor_copy, 256, HW)
         pts_products(0, accs0, (2, 3))
         pts_finish(0, accs0, (1,))
@@ -371,11 +386,15 @@ def tile_prefusioncat_kernel(
         w_copy("img", 2, 4, nc.vector.tensor_copy)
         pts_finish(1, accs1, (2,))
         pts_finish(1, accs1, (3,))
-        img_relu((0,))
+        img_relu((0,), (0,))
+        img_relu((0,), (1,))
         w_quant("img", 2, 4)
-        img_pad_cols(0)
-        img_pad_rows(0)
-        img_store(0)
+        img_pad_cols(0, 0, 1)
+        img_pad_cols(0, 1, 2)
+        img_pad_rows(0, 0, 1)
+        img_store(0, 0, 1)
+        img_pad_rows(0, 1, 2)
+        img_store(0, 1, 2)
         img_relu((1,))
         img_products(1)
         img_pad_cols(1)

@@ -148,25 +148,21 @@ def tile_prefusioncat_kernel(
         g10 = g1[:, 0:4]
 
         def spread_copy(dst, src):
-            nc.gpsimd.tensor_copy(out=dst, in_=src)
+            nc.gpsimd.tensor_scalar(out=dst, in0=src, scalar1=1.0, scalar2=0.0, op0=MUL, op1=ADD)
 
         def spread_cols0():
             spread_copy(ex0[:, :, 2:6, 4:12], g10)
-            spread_copy(
-                ex0[:, :, 2:6, :].rearrange("p t r (j c) -> p t r j c", c=4)[:, :, :, 0:4:3, :],
-                g10[:, :, :, 0:8:7].unsqueeze(4).to_broadcast([P, 4, 4, 2, 4]),
-            )
+            for lo, src in ((0, 0), (12, 7)):
+                spread_copy(ex0[:, :, 2:6, lo:lo + 4], g10[:, :, :, src:src + 1].to_broadcast([P, 4, 4, 4]))
 
         def spread_rows0():
-            spread_copy(
-                ex0[:].rearrange("p t (j r) c -> p t j r c", r=2)[:, :, 0:4:3, :, :],
-                ex0[:, :, 2:6:3, :].unsqueeze(3).to_broadcast([P, 4, 2, 2, 16]),
-            )
+            for lo, src in ((0, 2), (6, 5)):
+                spread_copy(ex0[:, :, lo:lo + 2, :], ex0[:, :, src:src + 1, :].to_broadcast([P, 4, 2, 16]))
 
         def spread_sample1():
             spread_copy(
-                ex1[:].rearrange("p a (b d) t -> p a b d t", d=2),
-                g1[:, 4:8].rearrange("p t a b -> p a b t").unsqueeze(3).to_broadcast([P, 4, 8, 2, 4]),
+                ex1[:].rearrange("p a (b d) t -> p (a b) d t", d=2),
+                g1[:, 4:8].rearrange("p t a b -> p (a b) t").unsqueeze(2).to_broadcast([P, 32, 2, 4]),
             )
 
         wt_ps = {}
@@ -334,10 +330,6 @@ def tile_prefusioncat_kernel(
 
         spread_cols0()
         bn_head("pts")
-        bn_s("pts", nc.gpsimd)
-        bn_dm("pts", nc.gpsimd)
-        bn_ds("pts", nc.gpsimd)
-        bn_t("pts", nc.gpsimd)
         spread_rows0()
         spread_sample1()
         w_transpose("pts", 0, 1)
@@ -354,8 +346,12 @@ def tile_prefusioncat_kernel(
         x_quant(0, 0, 256)
         x_quant(0, 256, HW)
         w_quant("pts", 0, 1)
+        bn_s("pts", nc.vector)
+        bn_dm("pts", nc.vector)
         w_quant("pts", 1, 2)
+        bn_ds("pts", nc.vector)
         w_quant("pts", 2, 3)
+        bn_t("pts", nc.vector)
         x_regroup(1, nc.vector.tensor_copy, 0, 256)
         pts_products(0, accs0, (0,))
         pts_products(0, accs0, (1,))

@@ -148,21 +148,25 @@ def tile_prefusioncat_kernel(
         g10 = g1[:, 0:4]
 
         def spread_copy(dst, src):
-            nc.gpsimd.tensor_scalar(out=dst, in0=src, scalar1=1.0, scalar2=0.0, op0=MUL, op1=ADD)
+            nc.gpsimd.tensor_copy(out=dst, in_=src)
 
         def spread_cols0():
             spread_copy(ex0[:, :, 2:6, 4:12], g10)
-            for lo, src in ((0, 0), (12, 7)):
-                spread_copy(ex0[:, :, 2:6, lo:lo + 4], g10[:, :, :, src:src + 1].to_broadcast([P, 4, 4, 4]))
+            spread_copy(
+                ex0[:, :, 2:6, :].rearrange("p t r (j c) -> p t r j c", c=4)[:, :, :, 0:4:3, :],
+                g10[:, :, :, 0:8:7].unsqueeze(4).to_broadcast([P, 4, 4, 2, 4]),
+            )
 
         def spread_rows0():
-            for lo, src in ((0, 2), (6, 5)):
-                spread_copy(ex0[:, :, lo:lo + 2, :], ex0[:, :, src:src + 1, :].to_broadcast([P, 4, 2, 16]))
+            spread_copy(
+                ex0[:].rearrange("p t (j r) c -> p t j r c", r=2)[:, :, 0:4:3, :, :],
+                ex0[:, :, 2:6:3, :].unsqueeze(3).to_broadcast([P, 4, 2, 2, 16]),
+            )
 
         def spread_sample1():
             spread_copy(
-                ex1[:].rearrange("p a (b d) t -> p (a b) d t", d=2),
-                g1[:, 4:8].rearrange("p t a b -> p (a b) t").unsqueeze(2).to_broadcast([P, 32, 2, 4]),
+                ex1[:].rearrange("p a (b d) t -> p a b d t", d=2),
+                g1[:, 4:8].rearrange("p t a b -> p a b t").unsqueeze(3).to_broadcast([P, 4, 8, 2, 4]),
             )
 
         wt_ps = {}

@@ -143,30 +143,21 @@ def tile_prefusioncat_kernel(
                     in1=g2v[:, :, src].unsqueeze(2).to_broadcast([P, 16, 2, hi - lo]), op=ADD,
                 )
 
-        ex0 = keep.tile([P, 4, 8, 16], F32, name="ex0")
+        ex0 = keep.tile([P, 4, 16, 4], F32, name="ex0")
         ex1 = keep.tile([P, 4, 16, 4], F32, name="ex1")
         g10 = g1[:, 0:4]
 
-        def spread_copy(dst, src):
-            nc.gpsimd.tensor_copy(out=dst, in_=src)
-
-        def spread_cols0():
-            spread_copy(ex0[:, :, 2:6, 4:12], g10)
-            spread_copy(
-                ex0[:, :, 2:6, :].rearrange("p t r (j c) -> p t r j c", c=4)[:, :, :, 0:4:3, :],
-                g10[:, :, :, 0:8:7].unsqueeze(4).to_broadcast([P, 4, 4, 2, 4]),
+        def spread_sample0():
+            nc.gpsimd.tensor_copy(out=ex0[:, :, 4:12, :], in_=g10.rearrange("p t a b -> p a b t"))
+            nc.gpsimd.tensor_copy(
+                out=ex0[:].rearrange("p a (j c) t -> p a j c t", c=4)[:, :, 0:4:3, :, :],
+                in_=g10[:, :, :, 0:8:7].rearrange("p t a j -> p a j t").unsqueeze(3).to_broadcast([P, 4, 2, 4, 4]),
             )
 
-        def spread_rows0():
-            spread_copy(
-                ex0[:].rearrange("p t (j r) c -> p t j r c", r=2)[:, :, 0:4:3, :, :],
-                ex0[:, :, 2:6:3, :].unsqueeze(3).to_broadcast([P, 4, 2, 2, 16]),
-            )
-
-        def spread_sample1():
-            spread_copy(
-                ex1[:].rearrange("p a (b d) t -> p a b d t", d=2),
-                g1[:, 4:8].rearrange("p t a b -> p a b t").unsqueeze(3).to_broadcast([P, 4, 8, 2, 4]),
+        def spread_sample1(copy_op):
+            copy_op(
+                out=ex1[:].rearrange("p a (b d) t -> p a b d t", d=2),
+                in_=g1[:, 4:8].rearrange("p t a b -> p a b t").unsqueeze(3).to_broadcast([P, 4, 8, 2, 4]),
             )
 
         wt_ps = {}
@@ -314,9 +305,12 @@ def tile_prefusioncat_kernel(
                 )
 
         def core_add():
-            nc.vector.tensor_tensor(
-                out=cg[:, 0], in0=f0[:, 0:4].rearrange("p t c -> p c t"), in1=ex0[:].rearrange("p t r s -> p (r s) t"), op=ADD,
-            )
+            for lo, hi, src in ((0, 3, slice(0, 1)), (3, 5, slice(1, 3)), (5, 8, slice(3, 4))):
+                nc.vector.tensor_tensor(
+                    out=cg[:, 0, 16 * lo:16 * hi, :].rearrange("p (r c) t -> p r c t", c=16),
+                    in0=f0[:, 0:4, 16 * lo:16 * hi].rearrange("p t (r c) -> p r c t", c=16),
+                    in1=ex0[:, src].to_broadcast([P, hi - lo, 16, 4]), op=ADD,
+                )
             nc.vector.tensor_tensor(
                 out=cg[:, 1].rearrange("p (a e m) t -> p a e m t", a=4, e=2),
                 in0=f0[:, 4:8].rearrange("p t (a e m) -> p a e m t", a=4, e=2),
@@ -332,10 +326,8 @@ def tile_prefusioncat_kernel(
         pyramid_2()
         pyramid_1()
 
-        spread_cols0()
+        spread_sample0()
         bn_head("pts")
-        spread_rows0()
-        spread_sample1()
         w_transpose("pts", 0, 1)
         w_transpose("pts", 1, 2)
         x_regroup(0, nc.vector.tensor_copy, 0, 256)
@@ -347,6 +339,7 @@ def tile_prefusioncat_kernel(
         w_copy("pts", 2, 3, nc.scalar.copy)
         w_transpose("pts", 3, 4)
         w_copy("pts", 3, 4, nc.scalar.copy)
+        spread_sample1(nc.scalar.copy)
         x_quant(0, 0, 256)
         x_quant(0, 256, HW)
         w_quant("pts", 0, 1)

@@ -147,9 +147,11 @@ def tile_prefusioncat_kernel(
         ex1 = keep.tile([P, 4, 16, 4], F32, name="ex1")
         g10 = g1[:, 0:4]
 
-        def spread_sample0():
-            nc.gpsimd.tensor_copy(out=ex0[:, :, 4:12, :], in_=g10.rearrange("p t a b -> p a b t"))
-            nc.gpsimd.tensor_copy(
+        def spread_mid0(copy_op):
+            copy_op(out=ex0[:, :, 4:12, :], in_=g10.rearrange("p t a b -> p a b t"))
+
+        def spread_sides0(copy_op):
+            copy_op(
                 out=ex0[:].rearrange("p a (j c) t -> p a j c t", c=4)[:, :, 0:4:3, :, :],
                 in_=g10[:, :, :, 0:8:7].rearrange("p t a j -> p a j t").unsqueeze(3).to_broadcast([P, 4, 2, 4, 4]),
             )
@@ -326,13 +328,14 @@ def tile_prefusioncat_kernel(
         pyramid_2()
         pyramid_1()
 
-        spread_sample0()
         bn_head("pts")
         w_transpose("pts", 0, 1)
         w_transpose("pts", 1, 2)
         x_regroup(0, nc.vector.tensor_copy, 0, 256)
         x_regroup(0, nc.scalar.copy, 320, HW)
         x_regroup(0, nc.vector.tensor_copy, 256, 320)
+        spread_mid0(nc.scalar.copy)
+        spread_sides0(nc.vector.tensor_copy)
         w_copy("pts", 0, 1, nc.scalar.copy)
         w_copy("pts", 1, 2, nc.scalar.copy)
         w_transpose("pts", 2, 3)

@@ -360,8 +360,7 @@ def tile_prefusioncat_kernel(
         x_regroup(1, nc.vector.tensor_copy, 256, HW)
         pts_products(0, accs0, (2, 3))
         pts_finish(0, accs0, (1,))
-        pts_finish(0, accs0, (2,))
-        pts_finish(0, accs0, (3,))
+        pts_finish(0, accs0, (2, 3))
         w_transpose("img", 0, 2)
         x_quant(1, 0, 256)
         x_quant(1, 256, HW)
@@ -376,12 +375,10 @@ def tile_prefusioncat_kernel(
         core_quant()
         w_quant("img", 0, 2)
         w_transpose("img", 2, 4)
-        pts_finish(1, accs1, (0,))
-        pts_finish(1, accs1, (1,))
+        pts_finish(1, accs1, (0, 1))
         img_products(0)
         w_copy("img", 2, 4, nc.vector.tensor_copy)
-        pts_finish(1, accs1, (2,))
-        pts_finish(1, accs1, (3,))
+        pts_finish(1, accs1, (2, 3))
         img_relu((0,), (0,))
         img_relu((0,), (1,))
         w_quant("img", 2, 4)

@@ -361,18 +361,20 @@ def tile_prefusioncat_kernel(
         pts_products(0, accs0, (2, 3))
         pts_finish(0, accs0, (1,))
         pts_finish(0, accs0, (2, 3))
-        w_transpose("img", 0, 2)
+        w_transpose("img", 0, 1)
+        w_transpose("img", 1, 2)
+        w_copy("img", 0, 1, nc.scalar.copy)
         x_quant(1, 0, 256)
         x_quant(1, 256, HW)
+        bn_dm("img", nc.vector)
         core_add()
         bn_head("img")
-        bn_dm("img", nc.gpsimd)
-        bn_s("img", nc.gpsimd)
-        bn_ds("img", nc.gpsimd)
-        bn_t("img", nc.gpsimd)
+        bn_s("img", nc.vector)
         pts_products(1, accs1, (0, 1, 2, 3))
-        w_copy("img", 0, 2, nc.vector.tensor_copy)
+        w_copy("img", 1, 2, nc.vector.tensor_copy)
+        bn_ds("img", nc.vector)
         core_quant()
+        bn_t("img", nc.vector)
         w_quant("img", 0, 2)
         w_transpose("img", 2, 4)
         pts_finish(1, accs1, (0, 1))

from contextlib import ExitStack

import concourse.mybir as mybir
from concourse.masks import make_identity

F32 = mybir.dt.float32
BF16 = mybir.dt.bfloat16
U32 = mybir.dt.uint32
U8 = mybir.dt.uint8
FP8X4 = mybir.dt.float8_e4m3fn_x4
ADD = mybir.AluOpType.add
SUB = mybir.AluOpType.subtract
MUL = mybir.AluOpType.mult
ACT = mybir.ActivationFunctionType

P = 128
NS = 2
C = 512
O = 512
OT = O // P
HW = 512
BN_EPS = 1e-5
FLOPS = 2 * 2 * O * C * NS * HW


def tile_prefusioncat_kernel(
    tc,
    img_feat0, img_feat1, img_feat2, img_feat3, img_feat4, pts_feat0,
    img_w, img_b, img_gamma, img_beta, img_mean, img_var,
    pts_w, pts_b, pts_gamma, pts_beta, pts_mean, pts_var,
    out,
):
    nc = tc.nc
    out_v = out.rearrange("n (b p a) h w -> n b p a (h w)", b=2, a=OT)
    with ExitStack() as ctx:
        keep = ctx.enter_context(tc.tile_pool(name="keep", bufs=1))
        ypool = ctx.enter_context(tc.tile_pool(name="ypool", bufs=8))
        psw = ctx.enter_context(tc.psum_pool(name="psw", bufs=3))
        pso = ctx.enter_context(tc.psum_pool(name="pso", bufs=5))

        ctx.enter_context(tc.manual_schedule())
        ident_f = keep.tile([P, P], F32, name="ident_f")
        make_identity(nc, ident_f[:])

        w_raw = {"pts": keep.tile([P, OT, C], BF16, name="w_raw_pts"), "img": keep.tile([P, OT, C], BF16, name="w_raw_img")}
        x_raw = [keep.tile([P, 4, HW], BF16, name="x_raw%d" % n) for n in range(NS)]
        sizes = (128, 32, 8, 2, 1)
        feats = (img_feat0, img_feat1, img_feat2, img_feat3, img_feat4)
        f_raw = [keep.tile([P, 2 * 4, sizes[lvl]], BF16, name="f_raw%d" % lvl) for lvl in range(5)]
        par = {"pts": keep.tile([P, 5, 16], BF16, name="par_pts"), "img": keep.tile([P, 5, 16], BF16, name="par_img")}
        vecs = {
            "pts": (pts_var, pts_gamma, pts_b, pts_mean, pts_beta),
            "img": (img_var, img_gamma, img_b, img_mean, img_beta),
        }

        def load_feat(eng, lvl):
            eng.dma_start(
                out=f_raw[lvl][:].rearrange("p (n t) s -> p n (t s)", n=NS),
                in_=feats[lvl].rearrange("n (p t) h w -> p n (t h w)", t=4),
            )

        def load_par(eng, br, q):
            eng.dma_start(out=par[br][:, q, 0:OT], in_=vecs[br][q].rearrange("(p a) -> p a", a=OT))

        def load_x(n):
            nc.sync.dma_start(out=x_raw[n][:], in_=pts_feat0[n].rearrange("(p t) h w -> p t (h w)", t=4))

        pts_w_v = pts_w.rearrange("(p a) c -> p a c", a=OT)
        img_w_v = img_w.rearrange("(p a) c -> p a c", a=OT)
        w_views = {"pts": pts_w_v, "img": img_w_v}

        def load_w(br, lo, hi):
            nc.sync.dma_start(out=w_raw[br][:, lo:hi, :], in_=w_views[br][:, lo:hi, :])

        load_feat(nc.sync, 4)
        load_feat(nc.scalar, 2)
        load_feat(nc.sync, 3)
        load_feat(nc.scalar, 1)
        load_par(nc.scalar, "pts", 0)
        load_x(0)
        load_w("pts", 0, 2)
        load_w("pts", 2, 4)
        for q in range(1, 5):
            load_par(nc.sync, "pts", q)
        load_x(1)
        load_feat(nc.sync, 0)
        load_w("img", 0, 2)
        load_w("img", 2, 4)
        for q in range(5):
            load_par(nc.sync, "img", q)
        eps = keep.tile([P, 1], F32, name="eps")
        nc.vector.memset(eps[:], BN_EPS)
        warm = keep.tile([P, 1], F32, name="warm")
        nc.scalar.activation(out=warm[:], in_=eps[:], func=ACT.Abs_reciprocal_sqrt)

        bn = {}

        def bn_tile(br, nm):
            bn[(br, nm)] = keep.tile([P, OT], F32, name=nm + "_" + br)
            return bn[(br, nm)]

        def bn_head(br):
            nc.scalar.activation(
                out=bn_tile(br, "rs")[:], in_=par[br][:, 0, 0:OT], func=ACT.Abs_reciprocal_sqrt, bias=eps[:], scale=1.0,
            )

        def bn_dm(br, eng):
            eng.tensor_tensor(out=bn_tile(br, "dm")[:], in0=par[br][:, 2, 0:OT], in1=par[br][:, 3, 0:OT], op=SUB)

        def bn_s(br, eng):
            eng.tensor_tensor(out=bn_tile(br, "s")[:], in0=par[br][:, 1, 0:OT], in1=bn[(br, "rs")][:], op=MUL)

        def bn_ds(br, eng):
            eng.tensor_tensor(out=bn_tile(br, "ds")[:], in0=bn[(br, "dm")][:], in1=bn[(br, "s")][:], op=MUL)

        def bn_t(br, eng):
            eng.tensor_tensor(out=bn_tile(br, "t")[:], in0=bn[(br, "ds")][:], in1=par[br][:, 4, 0:OT], op=ADD)

        f0, f1, f2, f3, f4 = f_raw
        g3x = keep.tile([P, 8, 2, 2], F32, name="g3x")
        g2 = keep.tile([P, 8, 2, 4], F32, name="g2")
        g1 = keep.tile([P, 8, 4, 8], F32, name="g1")

        def pyramid_34():
            nc.vector.tensor_tensor(
                out=g3x[:], in0=f3[:].unsqueeze(3).to_broadcast([P, 8, 2, 2]),
                in1=f4[:].unsqueeze(3).to_broadcast([P, 8, 2, 2]), op=ADD,
            )

        def pyramid_2():
            nc.vector.tensor_tensor(
                out=g2[:], in0=f2[:].rearrange("p q (a b) -> p q a b", a=2),
                in1=g3x[:].rearrange("p q b e -> p q (b e)").unsqueeze(2).to_broadcast([P, 8, 2, 4]), op=ADD,
            )

        def pyramid_1():
            g1v = g1[:].rearrange("p q (a e) b -> p (q a) e b", e=2)
            f1v = f1[:].rearrange("p q (a e b) -> p (q a) e b", e=2, b=8)
            g2v = g2[:].rearrange("p q a b -> p (q a) b")
            for lo, hi, src in ((2, 6, slice(0, 4)), (0, 2, slice(0, 1)), (6, 8, slice(3, 4))):
                nc.vector.tensor_tensor(
                    out=g1v[:, :, :, lo:hi], in0=f1v[:, :, :, lo:hi],
                    in1=g2v[:, :, src].unsqueeze(2).to_broadcast([P, 16, 2, hi - lo]), op=ADD,
                )

        ex0 = keep.tile([P, 4, 16, 4], F32, name="ex0")
        ex1 = keep.tile([P, 4, 16, 4], F32, name="ex1")
        g10 = g1[:, 0:4]

        def spread_mid0(copy_op):
            copy_op(out=ex0[:, :, 4:12, :], in_=g10.rearrange("p t a b -> p a b t"))

        def spread_sides0(copy_op):
            copy_op(
                out=ex0[:].rearrange("p a (j c) t -> p a j c t", c=4)[:, :, 0:4:3, :, :],
                in_=g10[:, :, :, 0:8:7].rearrange("p t a j -> p a j t").unsqueeze(3).to_broadcast([P, 4, 2, 4, 4]),
            )

        def spread_sample1(copy_op):
            copy_op(
                out=ex1[:].rearrange("p a (b d) t -> p a b d t", d=2),
                in_=g1[:, 4:8].rearrange("p t a b -> p a b t").unsqueeze(3).to_broadcast([P, 4, 8, 2, 4]),
            )

        wt_ps = {}
        wgt = {}
        for br in ("pts", "img"):
            wgt[br] = (
                keep.tile([P, OT * P * 4], BF16, name="wg_" + br, align_bytes=64),
                keep.tile([P, O], U32, name="wq_" + br, align_bytes=64),
                keep.tile([P, O], U8, name="ws_" + br, align_bytes=64),
            )

        def w_transpose(br, lo, hi):
            words = w_raw[br][:].bitcast(F32).rearrange("p a (m u) -> p a u m", u=2)
            wt = psw.tile([P, hi - lo, 2, P], F32, name="wt")
            for a in range(lo, hi):
                for u in range(2):
                    nc.tensor.transpose(wt[:, a - lo, u, :], words[:, a, u, :], ident_f[:])
            wt_ps[(br, lo)] = wt

        def w_copy(br, lo, hi, copy_out):
            wg_w = wgt[br][0][:].bitcast(F32).rearrange("p (a o u) -> p a o u", a=OT, u=2)
            copy_out(out=wg_w[:, lo:hi], in_=wt_ps[(br, lo)][:].rearrange("p a u o -> p a o u"))

        def w_quant(br, lo, hi):
            wg, wq, ws = wgt[br]
            nc.vector.quantize_mx(
                out=wq[:, lo * P:hi * P].bitcast(FP8X4), scales=ws[:, lo * P:hi * P],
                in_=wg[:, lo * 4 * P:hi * 4 * P],
            )

        xt = [
            (
                keep.tile([P, HW, 4], BF16, name="xg%d" % n, align_bytes=64),
                keep.tile([P, HW], U32, name="xq%d" % n, align_bytes=64),
                keep.tile([P, HW], U8, name="xs%d" % n, align_bytes=64),
            )
            for n in range(NS)
        ]

        def x_regroup(n, copy_op, lo, hi):
            copy_op(
                out=xt[n][0][:, lo:hi, :].rearrange("p (c i) t -> p c t i", i=4),
                in_=x_raw[n][:, :, lo:hi].rearrange("p t (c i) -> p c t i", i=4),
            )

        def x_quant(n, lo=0, hi=HW):
            xg, xq, xs = xt[n]
            nc.vector.quantize_mx(
                out=xq[:, lo:hi].bitcast(FP8X4), scales=xs[:, lo:hi], in_=xg[:, lo:hi, :].rearrange("p c t -> p (c t)"),
            )

        def product(acc, br, a, rq, rs_):
            wq, ws = wgt[br][1], wgt[br][2]
            nc.tensor.matmul_mx(
                out=acc,
                lhsT=wq[:, a * P:(a + 1) * P].bitcast(FP8X4), lhsT_scale=ws[:, a * P:(a + 1) * P],
                rhs=rq.bitcast(FP8X4), rhs_scale=rs_,
                start=True, stop=True,
            )

        def relu(br, a, dst, src):
            nc.scalar.activation(
                out=dst, in_=src, func=ACT.Relu,
                bias=bn[(br, "t")][:, a:a + 1], scale=bn[(br, "s")][:, a:a + 1],
            )

        def pts_products(n, accs, tiles):
            for a in tiles:
                acc = pso.tile([P, HW], F32, name="acc")
                product(acc[:], "pts", a, xt[n][1][:], xt[n][2][:])
                accs[a] = acc

        def pts_finish(n, accs, tiles):
            y = ypool.tile([P, 2, HW], F32, name="y")
            for k, a in enumerate(tiles):
                relu("pts", a, y[:, k, :], accs[a][:])
            nc.sync.dma_start(out=out_v[n, 1, :, tiles[0]:tiles[-1] + 1, :], in_=y[:, 0:len(tiles), :])

        def half_products(h):
            acc = pso.tile([P, 2, HW // 2], F32, name="acc")
            cols = slice(h * HW // 2, (h + 1) * HW // 2)
            for a in range(2):
                product(acc[:, a, :], "pts", a, xt[0][1][:, cols], xt[0][2][:, cols])
            half_acc[h] = acc

        def half_finish(h):
            y = ypool.tile([P, 2, HW // 2], F32, name="yh")
            cols = slice(h * HW // 2, (h + 1) * HW // 2)
            for a in range(2):
                relu("pts", a, y[:, a, :], half_acc[h][:, a, :])
            nc.sync.dma_start(out=out_v[0, 1, :, 0:2, cols], in_=y[:])

        half_acc = {}

        cg = keep.tile([P, NS, P, 4], BF16, name="cg", align_bytes=64)
        cq = keep.tile([P, NS * P], U32, name="cq", align_bytes=64)
        cs = keep.tile([P, NS * P], U8, name="cs", align_bytes=64)
        img_acc = {}
        img_out = {}

        def img_products(h):
            acc = pso.tile([P, 2, NS * P], F32, name="acc")
            for k in range(2):
                product(acc[:, k, :], "img", 2 * h + k, cq[:], cs[:])
                img_acc[2 * h + k] = acc[:, k, :]

        def img_relu(tiles, samples=(0, 1)):
            if tiles[0] not in img_out:
                img_out[tiles[0]] = keep.tile([P, NS, len(tiles), 16, 32], F32, name="fi%d" % tiles[0])
            fi = img_out[tiles[0]]
            lo, hi = samples[0], samples[-1] + 1
            for k, a in enumerate(tiles):
                relu(
                    "img", a, fi[:, lo:hi, k, 4:12, 8:24],
                    img_acc[a].rearrange("p (n r s) -> p n r s", n=NS, s=16)[:, lo:hi],
                )

        def img_pad_cols(a, lo=0, hi=NS):
            fi = img_out[a]
            g = (hi - lo) * fi.shape[2]
            fv = fi[:, lo:hi].rearrange("p n k r s -> p (n k) r s")
            nc.vector.tensor_copy(
                out=fv.rearrange("p g r (j c) -> p g r j c", c=8)[:, :, 4:12, 0:4:3, :],
                in_=fv[:, :, 4:12, 8:24:15].unsqueeze(4).to_broadcast([P, g, 8, 2, 8]),
            )

        def img_pad_rows(a, lo=0, hi=NS):
            fi = img_out[a]
            g = (hi - lo) * fi.shape[2]
            fv = fi[:, lo:hi].rearrange("p n k r s -> p (n k) r s")
            nc.vector.tensor_copy(
                out=fv.rearrange("p g (j c) s -> p g j c s", c=4)[:, :, 0:4:3, :, :],
                in_=fv[:, :, 4:12:7, :].unsqueeze(3).to_broadcast([P, g, 2, 4, 32]),
            )

        def img_pad(a):
            img_pad_cols(a)
            img_pad_rows(a)

        def img_store(a, lo=0, hi=NS):
            fi = img_out[a]
            for n in range(lo, hi):
                nc.sync.dma_start(
                    out=out_v[n, 0, :, a:a + fi.shape[2], :], in_=fi[:, n].rearrange("p k r s -> p k (r s)"),
                )

        def core_add():
            for lo, hi, src in ((0, 3, slice(0, 1)), (3, 5, slice(1, 3)), (5, 8, slice(3, 4))):
                nc.vector.tensor_tensor(
                    out=cg[:, 0, 16 * lo:16 * hi, :].rearrange("p (r c) t -> p r c t", c=16),
                    in0=f0[:, 0:4, 16 * lo:16 * hi].rearrange("p t (r c) -> p r c t", c=16),
                    in1=ex0[:, src].to_broadcast([P, hi - lo, 16, 4]), op=ADD,
                )
            nc.vector.tensor_tensor(
                out=cg[:, 1].rearrange("p (a e m) t -> p a e m t", a=4, e=2),
                in0=f0[:, 4:8].rearrange("p t (a e m) -> p a e m t", a=4, e=2),
                in1=ex1[:].unsqueeze(2).to_broadcast([P, 4, 2, 16, 4]), op=ADD,
            )

        def core_quant():
            nc.vector.quantize_mx(out=cq[:].bitcast(FP8X4), scales=cs[:], in_=cg[:].rearrange("p n c t -> p (n c t)"))

        accs0 = {}
        accs1 = {}
        pyramid_34()
        pyramid_2()
        pyramid_1()

        bn_head("pts")
        w_transpose("pts", 0, 1)
        w_transpose("pts", 1, 2)
        x_regroup(0, nc.vector.tensor_copy, 0, 256)
        x_regroup(0, nc.scalar.copy, 320, HW)
        x_regroup(0, nc.vector.tensor_copy, 256, 320)
        spread_mid0(nc.scalar.copy)
        spread_sides0(nc.vector.tensor_copy)
        w_copy("pts", 0, 1, nc.scalar.copy)
        w_copy("pts", 1, 2, nc.scalar.copy)
        w_transpose("pts", 2, 3)
        w_copy("pts", 2, 3, nc.scalar.copy)
        w_transpose("pts", 3, 4)
        w_copy("pts", 3, 4, nc.scalar.copy)
        spread_sample1(nc.scalar.copy)
        x_quant(0, 0, 256)
        x_quant(0, 256, HW)
        w_quant("pts", 0, 1)
        bn_s("pts", nc.vector)
        bn_dm("pts", nc.vector)
        w_quant("pts", 1, 2)
        bn_ds("pts", nc.vector)
        w_quant("pts", 2, 3)
        bn_t("pts", nc.vector)
        x_regroup(1, nc.vector.tensor_copy, 0, 256)
        pts_products(0, accs0, (0,))
        pts_products(0, accs0, (1,))
        pts_finish(0, accs0, (0,))
        w_quant("pts", 3, 4)
        x_regroup(1, nc.vector.tensor_copy, 256, HW)
        pts_products(0, accs0, (2, 3))
        pts_finish(0, accs0, (1,))
        pts_finish(0, accs0, (2, 3))
        w_transpose("img", 0, 1)
        w_transpose("img", 1, 2)
        w_copy("img", 0, 1, nc.scalar.copy)
        x_quant(1, 0, 256)
        x_quant(1, 256, HW)
        bn_dm("img", nc.vector)
        core_add()
        bn_head("img")
        bn_s("img", nc.vector)
        pts_products(1, accs1, (0, 1, 2, 3))
        w_copy("img", 1, 2, nc.vector.tensor_copy)
        bn_ds("img", nc.vector)
        core_quant()
        bn_t("img", nc.vector)
        w_quant("img", 0, 2)
        w_transpose("img", 2, 4)
        pts_finish(1, accs1, (0, 1))
        img_products(0)
        w_copy("img", 2, 4, nc.vector.tensor_copy)
        pts_finish(1, accs1, (2, 3))
        img_relu((0,), (0,))
        img_relu((0,), (1,))
        w_quant("img", 2, 4)
        img_pad_cols(0, 0, 1)
        img_pad_cols(0, 1, 2)
        img_pad_rows(0, 0, 1)
        img_store(0, 0, 1)
        img_pad_rows(0, 1, 2)
        img_store(0, 1, 2)
        img_relu((1,))
        img_products(1)
        img_pad_cols(1)
        img_relu((2, 3))
        img_pad_rows(1)
        img_store(1)
        img_pad_cols(2)
        img_pad_rows(2)
        img_store(2)
